import numpy as np
import ml_dtypes


def mxq(x, axis, fmt="e4m3"):
    dtype, down = {"e4m3": (ml_dtypes.float8_e4m3fn, 7), "e5m2": (ml_dtypes.float8_e5m2, 14)}[fmt]
    v = np.moveaxis(np.asarray(x, np.float32).astype(ml_dtypes.bfloat16).astype(np.float64), axis, -1)
    blocks = v.reshape(v.shape[:-1] + (-1, 32))
    amax = np.abs(blocks).max(-1, keepdims=True)
    byte = np.maximum(np.where(amax > 0, np.frexp(amax)[1] - 1 + 127, 0) - down, 1)
    scale = np.exp2(byte - 127.0)
    codes = (blocks / scale).astype(np.float32).astype(dtype).astype(np.float64)
    return np.moveaxis((codes * scale).reshape(v.shape), -1, axis)


WIDE = False


def mx_kscale(k):
    if not WIDE:
        return np.ones(k)
    levels = np.array([10, -10, 5, -5, 0])
    a = np.random.permutation(np.resize(levels, k // 512 * 4)).reshape(k // 512, 4)
    idx = np.arange(k)
    return np.exp2(a[idx // 512, idx % 128 // 32])


BF16 = ml_dtypes.bfloat16


def bf(x):
    return np.asarray(x, np.float32).astype(BF16)


def f64(x):
    return np.asarray(x).astype(np.float64)


E2M1 = np.array([0.0, 0.5, 1.0, 1.5, 2.0, 3.0, 4.0, 6.0, -0.0, -0.5, -1.0, -1.5, -2.0, -3.0, -4.0, -6.0])


def pack_weight(w, fmt):
    k, n = w.shape
    w = f64(bf(w)).reshape(k // 32, 32, n)
    amax = np.abs(w).max(1)
    if fmt == "e4m3":
        byte = np.frexp(amax)[1] - 1 + 127 - 7
    else:
        mant, ex = np.frexp(amax / 6.0)
        byte = np.where(mant > 0.5, ex, ex - 1) + 127
    byte = np.clip(np.where(amax > 0, byte, 1), 1, 254)
    scaled = (w * np.exp2(127.0 - byte)[:, None, :]).reshape(k, n).astype(np.float32)
    by_word = np.ascontiguousarray(scaled.reshape(k // 512, 128, 4, n).transpose(0, 1, 3, 2))
    if fmt == "e4m3":
        words = by_word.astype(ml_dtypes.float8_e4m3fn).view(np.uint8)
    else:
        c = by_word.astype(ml_dtypes.float4_e2m1fn).view(np.uint8) & 0xF
        words = c[..., 0::2] | (c[..., 1::2] << 4)
    return np.ascontiguousarray(words), np.ascontiguousarray(byte.astype(np.uint8).reshape(k // 512, 16, n))


def unpack_weight(words, scales, fmt):
    g, p, n, _ = words.shape
    if fmt == "e4m3":
        vals = np.ascontiguousarray(words).view(ml_dtypes.float8_e4m3fn).astype(np.float64)
    else:
        nib = np.empty((g, p, n, 4), np.uint8)
        nib[..., 0::2] = words & 0xF
        nib[..., 1::2] = words >> 4
        vals = E2M1[nib]
    vals = vals * np.repeat(np.exp2(scales.astype(np.float64) - 127.0), 8, axis=1)[..., None]
    return vals.transpose(0, 1, 3, 2).reshape(g * 512, n)


N, T, D, B0, C, P0, V1, P1, V2 = 2, 512, 1024, 2046, 2, 512, 2048, 512, 1024
MU = 0.25
SIG = 2.0
FMT = "e4m3"


def softmax(v):
    e = np.exp(v - v.max(-1, keepdims=True))
    return e / e.sum(-1, keepdims=True)


def setup_inputs():
    s, t = mx_kscale(D), mx_kscale(P0)
    hw = np.random.standard_normal((D, B0 + C)) * SIG / np.sqrt(D)
    hw[:, B0:] = hw[:, B0:] / SIG + (np.log(B0) + 0.5 * SIG * SIG) / (MU * D)
    x = bf((np.random.standard_normal((N, T, D)) + MU) * s)
    head_words, head_scales = pack_weight(hw / s[:, None], FMT)
    proj_words, proj_scales = pack_weight(np.random.standard_normal((D, P0)) / np.sqrt(D) / s[:, None] * t, FMT)
    tail_words, tail_scales = pack_weight(np.random.standard_normal((P0, V1)) * SIG / np.sqrt(P0) / t[:, None], FMT)
    return {"x": x,
            "head_weight_words": head_words, "head_weight_scales": head_scales,
            "tail_proj_0_words": proj_words, "tail_proj_0_scales": proj_scales,
            "tail_w_0_words": tail_words, "tail_w_0_scales": tail_scales}


def reference(x, head_weight_words, head_weight_scales, tail_proj_0_words, tail_proj_0_scales, tail_w_0_words, tail_w_0_scales):
    xq = mxq(f64(x), 2, "e4m3")
    head_sm = softmax(xq @ unpack_weight(head_weight_words, head_weight_scales, FMT))
    h = xq @ unpack_weight(tail_proj_0_words, tail_proj_0_scales, FMT)
    tail_sm = softmax(mxq(h, 2, "e4m3") @ unpack_weight(tail_w_0_words, tail_w_0_scales, FMT))
    probs = np.concatenate([head_sm[..., :B0], tail_sm * head_sm[..., B0:B0 + 1]], axis=-1)
    return probs, head_sm[..., B0 + 1:B0 + C]

@@ -1,0 +1,309 @@
+from contextlib import ExitStack
+
+import concourse.mybir as mybir
+from concourse.masks import make_identity
+
+F32 = mybir.dt.float32
+BF16 = mybir.dt.bfloat16
+I32 = mybir.dt.int32
+U32 = mybir.dt.uint32
+U8 = mybir.dt.uint8
+FP8X4 = mybir.dt.float8_e4m3fn_x4
+ALU = mybir.AluOpType
+ACT = mybir.ActivationFunctionType
+AXIS = mybir.AxisListType
+
+P = 128
+PACK = 4
+K_PASS = P * PACK
+BANK = 512
+
+TOKENS = 1024
+TILES = TOKENS // P
+D = 1024
+X_PASSES = D // K_PASS
+H = 512
+VOCAB = 2048
+ROW_BANKS = VOCAB // BANK
+HEAD_TOKENS = VOCAB - 2
+
+HEAD_PLANE = (0, 4)
+TAIL_PLANE = 8
+PROJ_PLANE = 12
+
+FLOPS = 2 * TOKENS * (D * VOCAB + D * H + H * VOCAB)
+
+
+def tile_adaptiveinputsoftmax_pa_kernel(
+    tc,
+    x,
+    head_weight_words,
+    head_weight_scales,
+    tail_proj_0_words,
+    tail_proj_0_scales,
+    tail_w_0_words,
+    tail_w_0_scales,
+    out_0,
+    out_1,
+):
+    nc = tc.nc
+    x_rows = x.flatten_outer_dims()
+    probs = out_0.flatten_outer_dims()
+    other_cluster = out_1.rearrange("n (a p) o -> (n a) (p o)", p=P)
+
+    with ExitStack() as ctx:
+        keep = ctx.enter_context(tc.tile_pool(name="keep", bufs=1))
+        stage = ctx.enter_context(tc.tile_pool(name="stage", bufs=3))
+        small = ctx.enter_context(tc.tile_pool(name="small", bufs=4))
+        rows_pool = ctx.enter_context(tc.tile_pool(name="rows", bufs=8))
+        psum = ctx.enter_context(tc.psum_pool(name="psum", bufs=8))
+
+        x_sb = keep.tile([P, TILES, D], BF16)
+        x_codes = keep.tile([P, TILES * X_PASSES * P], U32, align_bytes=64)
+        x_scales = keep.tile([P, TILES * X_PASSES * P], U8, align_bytes=64)
+        h_codes = keep.tile([P, TILES * P], U32, align_bytes=64)
+        h_scales = keep.tile([P, TILES * P], U8, align_bytes=64)
+        head_w = keep.tile([P, X_PASSES, VOCAB], U32, align_bytes=64)
+        proj_w = keep.tile([P, X_PASSES, H], U32, align_bytes=64)
+        tail_w = keep.tile([P, VOCAB], U32, align_bytes=64)
+        planes = keep.tile([P, VOCAB], U8, align_bytes=64)
+        ident_f32 = keep.tile([P, P], F32)
+        ident_bf16 = keep.tile([P, P], BF16)
+        clusters = keep.tile([P, P], F32)
+        clusters_t = keep.tile([P, P], F32)
+
+        nc.vector.memset(planes[:].bitcast(I32), 0)
+        nc.vector.memset(clusters[:], 0.0)
+
+        for i in range(TILES):
+            nc.scalar.dma_start(out=x_sb[:, i, :], in_=x_rows[i * P : (i + 1) * P, :])
+
+        for q in range(4):
+            nc.sync.dma_start(
+                out=planes[32 * q + PROJ_PLANE : 32 * q + PROJ_PLANE + 4, 0 : X_PASSES * H]
+                .bitcast(I32)
+                .rearrange("r (g n) -> r g n", g=X_PASSES),
+                in_=tail_proj_0_scales[:, 4 * q : 4 * q + 4, :].bitcast(I32).rearrange("g r n -> r g n"),
+            )
+        for q in range(4):
+            nc.sync.dma_start(
+                out=planes[32 * q + HEAD_PLANE[0] : 32 * q + HEAD_PLANE[0] + 8, :].bitcast(I32),
+                in_=head_weight_scales[:, 4 * q : 4 * q + 4, :].bitcast(I32),
+            )
+        for q in range(4):
+            nc.sync.dma_start(
+                out=planes[32 * q + TAIL_PLANE : 32 * q + TAIL_PLANE + 4, :].bitcast(I32),
+                in_=tail_w_0_scales[0, 4 * q : 4 * q + 4, :].bitcast(I32),
+            )
+        nc.sync.dma_start(
+            out=proj_w[:].bitcast(I32),
+            in_=tail_proj_0_words.rearrange("g p n t -> p g (n t)").bitcast(I32),
+        )
+        head_words = head_weight_words.rearrange("g p n t -> p g (n t)")
+        for c in range(ROW_BANKS):
+            nc.sync.dma_start(
+                out=head_w[:, :, c * BANK : (c + 1) * BANK].bitcast(I32),
+                in_=head_words[:, :, c * BANK * PACK : (c + 1) * BANK * PACK].bitcast(I32),
+            )
+        tail_words = tail_w_0_words[0].rearrange("p n t -> p (n t)")
+        for c in range(ROW_BANKS):
+            nc.sync.dma_start(
+                out=tail_w[:, c * BANK : (c + 1) * BANK].bitcast(I32),
+                in_=tail_words[:, c * BANK * PACK : (c + 1) * BANK * PACK].bitcast(I32),
+            )
+
+        make_identity(nc, ident_f32[:])
+        make_identity(nc, ident_bf16[:])
+
+        zero = small.tile([P, 1], F32)
+        one = small.tile([P, 1], F32)
+        nc.vector.memset(zero[:], 0.0)
+        nc.scalar.activation(out=one[:], in_=zero[:], func=ACT.Exp)
+
+        def transpose_x(i):
+            words = x_sb[:, i, :].bitcast(F32)
+            half = K_PASS // 2
+            xt = psum.tile([P, X_PASSES, 2, P], F32, tag="bank")
+            for g in range(X_PASSES):
+                for u in range(2):
+                    nc.tensor.transpose(
+                        xt[:, g, u, :], words[:, g * half + u : (g + 1) * half : 2], ident_f32[:]
+                    )
+            grouped = stage.tile([P, D], BF16, align_bytes=64, tag="x_grouped")
+            copy = nc.vector.tensor_copy if i % 2 == 0 else nc.scalar.copy
+            copy(
+                out=grouped[:].bitcast(F32).rearrange("p (g r u) -> p g r u", g=X_PASSES, u=2),
+                in_=xt[:].rearrange("p g u r -> p g r u"),
+            )
+            return grouped
+
+        def quantise_x(i, grouped):
+            cols = slice(i * X_PASSES * P, (i + 1) * X_PASSES * P)
+            nc.vector.quantize_mx(
+                out=x_codes[:, cols].bitcast(FP8X4), scales=x_scales[:, cols], in_=grouped[:]
+            )
+
+        def x_pass(i, g):
+            cols = slice((i * X_PASSES + g) * P, (i * X_PASSES + g + 1) * P)
+            return x_codes[:, cols], x_scales[:, cols]
+
+        def project(i, h_pair):
+            h_ps = psum.tile([P, H], F32, tag="bank")
+            for g in range(X_PASSES):
+                codes, scales = x_pass(i, g)
+                nc.tensor.matmul_mx(
+                    out=h_ps[:],
+                    lhsT=codes.bitcast(FP8X4),
+                    lhsT_scale=scales,
+                    rhs=proj_w[:, g, :].bitcast(FP8X4),
+                    rhs_scale=planes[PROJ_PLANE:P, g * H : (g + 1) * H],
+                    start=(g == 0),
+                    stop=(g == X_PASSES - 1),
+                )
+            nc.scalar.copy(out=h_pair[:, i % 2, :, :], in_=h_ps[:].rearrange("p (q t) -> p t q", t=PACK))
+
+        def transpose_h(j, h_pair):
+            ht = psum.tile([P, 2, PACK, P], BF16, tag="bank")
+            for a in range(2):
+                for t in range(PACK):
+                    nc.tensor.transpose(ht[:, a, t, :], h_pair[:, a, t, :], ident_bf16[:])
+            grouped = stage.tile([P, 2, P, PACK], BF16, align_bytes=64, tag="h_grouped")
+            nc.scalar.copy(out=grouped[:], in_=ht[:].rearrange("p a t r -> p a r t"))
+            cols = slice(2 * j * P, 2 * (j + 1) * P)
+            nc.vector.quantize_mx(
+                out=h_codes[:, cols].bitcast(FP8X4),
+                scales=h_scales[:, cols],
+                in_=grouped[:].rearrange("p a r t -> p (a r t)"),
+            )
+
+        def head_passes(i):
+            return [
+                x_pass(i, g) + (head_w[:, g, :], planes[HEAD_PLANE[g] : P, :]) for g in range(X_PASSES)
+            ]
+
+        def tail_passes(i):
+            cols = slice(i * P, (i + 1) * P)
+            return [(h_codes[:, cols], h_scales[:, cols], tail_w[:], planes[TAIL_PLANE:P, :])]
+
+        def logits(passes):
+            banks = []
+            for c in range(ROW_BANKS):
+                cols = slice(c * BANK, (c + 1) * BANK)
+                bank = psum.tile([P, BANK], F32, tag="bank")
+                for k, (codes, scales, w_words, w_scales) in enumerate(passes):
+                    nc.tensor.matmul_mx(
+                        out=bank[:],
+                        lhsT=codes.bitcast(FP8X4),
+                        lhsT_scale=scales,
+                        rhs=w_words[:, cols].bitcast(FP8X4),
+                        rhs_scale=w_scales[:, cols],
+                        start=(k == 0),
+                        stop=(k == len(passes) - 1),
+                    )
+                banks.append(bank)
+            return banks
+
+        def minus_row_max(banks):
+            bank_max = small.tile([P, ROW_BANKS], F32)
+            for c, bank in enumerate(banks):
+                nc.vector.reduce_max(out=bank_max[:, c : c + 1], in_=bank[:], axis=AXIS.X)
+            minus_max = small.tile([P, 1], F32)
+            nc.vector.tensor_reduce(out=minus_max[:], in_=bank_max[:], axis=AXIS.X, op=ALU.max, negate=True)
+            return minus_max
+
+        def exponentials(banks, minus_max):
+            row = rows_pool.tile([P, VOCAB], F32)
+            bank_sum = small.tile([P, ROW_BANKS], F32)
+            for c, bank in enumerate(banks):
+                nc.scalar.activation(
+                    out=row[:, c * BANK : (c + 1) * BANK],
+                    in_=bank[:],
+                    func=ACT.Exp,
+                    bias=minus_max[:],
+                    accum_out=bank_sum[:, c : c + 1],
+                )
+            return row, bank_sum
+
+        def one_over_sum(bank_sum):
+            total = small.tile([P, 1], F32)
+            nc.vector.reduce_sum(out=total[:], in_=bank_sum[:], axis=AXIS.X)
+            inverse = small.tile([P, 1], F32)
+            nc.vector.reciprocal(out=inverse[:], in_=total[:])
+            return inverse
+
+        def finish_head(i, row, bank_sum):
+            inverse = one_over_sum(bank_sum)
+            nc.vector.tensor_scalar(
+                out=clusters[:, i : 2 * TILES : TILES],
+                in0=row[:, HEAD_TOKENS:VOCAB],
+                scalar1=inverse[:],
+                scalar2=None,
+                op0=ALU.mult,
+            )
+            nc.gpsimd.tensor_scalar(
+                out=row[:, 0:HEAD_TOKENS],
+                in0=row[:, 0:HEAD_TOKENS],
+                scalar1=inverse[:],
+                scalar2=0.0,
+                op0=ALU.mult,
+                op1=ALU.add,
+            )
+            nc.sync.dma_start(out=probs[i * P : (i + 1) * P, 0:HEAD_TOKENS], in_=row[:, 0:HEAD_TOKENS])
+
+        def finish_tail(i, row, bank_sum):
+            inverse = one_over_sum(bank_sum)
+            nc.gpsimd.tensor_scalar(
+                out=row[:],
+                in0=row[:],
+                scalar1=inverse[:],
+                scalar2=clusters[:, i : i + 1],
+                op0=ALU.mult,
+                op1=ALU.mult,
+            )
+            nc.sync.dma_start(out=probs[i * P : (i + 1) * P, HEAD_TOKENS : HEAD_TOKENS + VOCAB], in_=row[:])
+
+        x_grouped = {}
+        for i in range(TILES):
+            x_grouped[i] = transpose_x(i)
+            if i >= 1:
+                quantise_x(i - 1, x_grouped[i - 1])
+        quantise_x(TILES - 1, x_grouped[TILES - 1])
+
+        h_pairs = {}
+        for i in range(TILES):
+            if i % 2 == 0:
+                h_pairs[i // 2] = stage.tile([P, 2, PACK, P], BF16, tag="h_pair", bufs=TILES // 2, name="h_pair")
+            project(i, h_pairs[i // 2])
+        for j in range(TILES // 2):
+            transpose_h(j, h_pairs[j])
+
+        softmaxes = 2 * TILES
+        banks = {}
+        done = {}
+
+        def start(u):
+            banks[u] = logits(head_passes(u // 2) if u % 2 == 0 else tail_passes(u // 2))
+
+        def finish(u):
+            row, bank_sum = done[u]
+            if u % 2 == 0:
+                finish_head(u // 2, row, bank_sum)
+            else:
+                finish_tail(u // 2, row, bank_sum)
+
+        start(0)
+        start(1)
+        for u in range(softmaxes):
+            minus_max = minus_row_max(banks[u])
+            done[u] = exponentials(banks[u], minus_max)
+            if u >= 1:
+                finish(u - 1)
+            if u + 2 < softmaxes:
+                start(u + 2)
+
+        ct = psum.tile([P, P], F32, tag="bank")
+        nc.tensor.transpose(ct[:], clusters[:], ident_f32[:])
+        nc.vector.tensor_copy(out=clusters_t[:], in_=ct[:])
+        nc.sync.dma_start(out=other_cluster, in_=clusters_t[TILES : 2 * TILES, :])
+
+        finish(softmaxes - 1)

@@ -240,19 +240,18 @@ def tile_adaptiveinputsoftmax_pa_kernel(
                 scalar2=None,
                 op0=ALU.mult,
             )
-            nc.gpsimd.tensor_scalar(
+            nc.vector.tensor_scalar(
                 out=row[:, 0:HEAD_TOKENS],
                 in0=row[:, 0:HEAD_TOKENS],
                 scalar1=inverse[:],
-                scalar2=0.0,
+                scalar2=None,
                 op0=ALU.mult,
-                op1=ALU.add,
             )
             nc.sync.dma_start(out=probs[i * P : (i + 1) * P, 0:HEAD_TOKENS], in_=row[:, 0:HEAD_TOKENS])
 
         def finish_tail(i, row, bank_sum):
             inverse = one_over_sum(bank_sum)
-            nc.gpsimd.tensor_scalar(
+            nc.vector.tensor_scalar(
                 out=row[:],
                 in0=row[:],
                 scalar1=inverse[:],

@@ -233,25 +233,25 @@ def tile_adaptiveinputsoftmax_pa_kernel(
 
         def finish_head(i, row, bank_sum):
             inverse = one_over_sum(bank_sum)
-            nc.vector.tensor_scalar(
+            nc.scalar.activation(
                 out=clusters[:, i : 2 * TILES : TILES],
-                in0=row[:, HEAD_TOKENS:VOCAB],
-                scalar1=inverse[:],
-                scalar2=None,
-                op0=ALU.mult,
+                in_=row[:, HEAD_TOKENS:VOCAB],
+                func=ACT.Copy,
+                scale=inverse[:],
             )
-            nc.vector.tensor_scalar(
+            nc.gpsimd.tensor_scalar(
                 out=row[:, 0:HEAD_TOKENS],
                 in0=row[:, 0:HEAD_TOKENS],
                 scalar1=inverse[:],
-                scalar2=None,
+                scalar2=0.0,
                 op0=ALU.mult,
+                op1=ALU.add,
             )
             nc.sync.dma_start(out=probs[i * P : (i + 1) * P, 0:HEAD_TOKENS], in_=row[:, 0:HEAD_TOKENS])
 
         def finish_tail(i, row, bank_sum):
             inverse = one_over_sum(bank_sum)
-            nc.vector.tensor_scalar(
+            nc.gpsimd.tensor_scalar(
                 out=row[:],
                 in0=row[:],
                 scalar1=inverse[:],

@@ -261,6 +261,18 @@ def tile_adaptiveinputsoftmax_pa_kernel(
             )
             nc.sync.dma_start(out=probs[i * P : (i + 1) * P, HEAD_TOKENS : HEAD_TOKENS + VOCAB], in_=row[:])
 
+        def finish_last_tail(i, row, bank_sum):
+            inverse = one_over_sum(bank_sum)
+            factor = small.tile([P, 1], F32)
+            nc.scalar.activation(out=factor[:], in_=inverse[:], func=ACT.Copy, scale=clusters[:, i : i + 1])
+            for half in range(2):
+                lo = half * VOCAB // 2
+                hi = lo + VOCAB // 2
+                nc.scalar.activation(out=row[:, lo:hi], in_=row[:, lo:hi], func=ACT.Copy, scale=factor[:])
+                nc.sync.dma_start(
+                    out=probs[i * P : (i + 1) * P, HEAD_TOKENS + lo : HEAD_TOKENS + hi], in_=row[:, lo:hi]
+                )
+
         x_grouped = {}
         for i in range(TILES):
             x_grouped[i] = transpose_x(i)
@@ -287,8 +299,10 @@ def tile_adaptiveinputsoftmax_pa_kernel(
             row, bank_sum = done[u]
             if u % 2 == 0:
                 finish_head(u // 2, row, bank_sum)
-            else:
+            elif u < softmaxes - 1:
                 finish_tail(u // 2, row, bank_sum)
+            else:
+                finish_last_tail(u // 2, row, bank_sum)
 
         start(0)
         start(1)

@@ -26,6 +26,8 @@ H = 512
 VOCAB = 2048
 ROW_BANKS = VOCAB // BANK
 HEAD_TOKENS = VOCAB - 2
+ROW = HEAD_TOKENS + VOCAB
+ALIGN = 8
 
 HEAD_PLANE = (0, 4)
 TAIL_PLANE = 8
@@ -47,15 +49,14 @@ def tile_adaptiveinputsoftmax_pa_kernel(
     out_1,
 ):
     nc = tc.nc
-    x_rows = x.flatten_outer_dims()
-    probs = out_0.flatten_outer_dims()
-    other_cluster = out_1.rearrange("n (a p) o -> (n a) (p o)", p=P)
+    x_rows = x.flatten_outer_dims().rearrange("(p i) d -> p i d", i=TILES)
+    probs = out_0.flatten_outer_dims().rearrange("(p i) c -> p (i c)", i=TILES)
+    other_cluster = out_1.rearrange("n t o -> (n t o)").rearrange("(p i) -> p i", i=TILES)
 
     with ExitStack() as ctx:
         keep = ctx.enter_context(tc.tile_pool(name="keep", bufs=1))
         stage = ctx.enter_context(tc.tile_pool(name="stage", bufs=3))
         small = ctx.enter_context(tc.tile_pool(name="small", bufs=4))
-        rows_pool = ctx.enter_context(tc.tile_pool(name="rows", bufs=8))
         psum = ctx.enter_context(tc.psum_pool(name="psum", bufs=8))
 
         x_sb = keep.tile([P, TILES, D], BF16)
@@ -69,14 +70,13 @@ def tile_adaptiveinputsoftmax_pa_kernel(
         planes = keep.tile([P, VOCAB], U8, align_bytes=64)
         ident_f32 = keep.tile([P, P], F32)
         ident_bf16 = keep.tile([P, P], BF16)
-        clusters = keep.tile([P, P], F32)
-        clusters_t = keep.tile([P, P], F32)
+        clusters = keep.tile([P, 2 * TILES], F32)
+        out_sb = keep.tile([P, TILES * ROW], F32)
 
         nc.vector.memset(planes[:].bitcast(I32), 0)
-        nc.vector.memset(clusters[:], 0.0)
 
         for i in range(TILES):
-            nc.scalar.dma_start(out=x_sb[:, i, :], in_=x_rows[i * P : (i + 1) * P, :])
+            nc.scalar.dma_start(out=x_sb[:, i, :], in_=x_rows[:, i, :])
 
         for q in range(4):
             nc.sync.dma_start(
@@ -211,8 +211,8 @@ def tile_adaptiveinputsoftmax_pa_kernel(
             nc.vector.tensor_reduce(out=minus_max[:], in_=bank_max[:], axis=AXIS.X, op=ALU.max, negate=True)
             return minus_max
 
-        def exponentials(banks, minus_max):
-            row = rows_pool.tile([P, VOCAB], F32)
+        def exponentials(banks, minus_max, first_col):
+            row = out_sb[:, first_col : first_col + VOCAB]
             bank_sum = small.tile([P, ROW_BANKS], F32)
             for c, bank in enumerate(banks):
                 nc.scalar.activation(
@@ -231,6 +231,15 @@ def tile_adaptiveinputsoftmax_pa_kernel(
             nc.vector.reciprocal(out=inverse[:], in_=total[:])
             return inverse
 
+        def down(col):
+            return col // ALIGN * ALIGN
+
+        def up(col):
+            return (col + ALIGN - 1) // ALIGN * ALIGN
+
+        def store(lo, hi):
+            nc.sync.dma_start(out=probs[:, lo:hi], in_=out_sb[:, lo:hi])
+
         def finish_head(i, row, bank_sum):
             inverse = one_over_sum(bank_sum)
             nc.scalar.activation(
@@ -247,19 +256,19 @@ def tile_adaptiveinputsoftmax_pa_kernel(
                 op0=ALU.mult,
                 op1=ALU.add,
             )
-            nc.sync.dma_start(out=probs[i * P : (i + 1) * P, 0:HEAD_TOKENS], in_=row[:, 0:HEAD_TOKENS])
+            store(up(i * ROW), down(i * ROW + HEAD_TOKENS))
 
         def finish_tail(i, row, bank_sum):
             inverse = one_over_sum(bank_sum)
             nc.gpsimd.tensor_scalar(
-                out=row[:],
-                in0=row[:],
+                out=row,
+                in0=row,
                 scalar1=inverse[:],
                 scalar2=clusters[:, i : i + 1],
                 op0=ALU.mult,
                 op1=ALU.mult,
             )
-            nc.sync.dma_start(out=probs[i * P : (i + 1) * P, HEAD_TOKENS : HEAD_TOKENS + VOCAB], in_=row[:])
+            store(down(i * ROW + HEAD_TOKENS), up((i + 1) * ROW))
 
         def finish_last_tail(i, row, bank_sum):
             inverse = one_over_sum(bank_sum)
@@ -269,9 +278,7 @@ def tile_adaptiveinputsoftmax_pa_kernel(
                 lo = half * VOCAB // 2
                 hi = lo + VOCAB // 2
                 nc.scalar.activation(out=row[:, lo:hi], in_=row[:, lo:hi], func=ACT.Copy, scale=factor[:])
-                nc.sync.dma_start(
-                    out=probs[i * P : (i + 1) * P, HEAD_TOKENS + lo : HEAD_TOKENS + hi], in_=row[:, lo:hi]
-                )
+                store(i * ROW + HEAD_TOKENS + lo, i * ROW + HEAD_TOKENS + hi)
 
         x_grouped = {}
         for i in range(TILES):
@@ -288,35 +295,39 @@ def tile_adaptiveinputsoftmax_pa_kernel(
         for j in range(TILES // 2):
             transpose_h(j, h_pairs[j])
 
-        softmaxes = 2 * TILES
+        order = [("head", 0)]
+        for i in range(TILES - 1):
+            order.extend([("head", i + 1), ("tail", i)])
+        order.append(("tail", TILES - 1))
+        softmaxes = len(order)
         banks = {}
         done = {}
 
         def start(u):
-            banks[u] = logits(head_passes(u // 2) if u % 2 == 0 else tail_passes(u // 2))
+            kind, i = order[u]
+            banks[u] = logits(head_passes(i) if kind == "head" else tail_passes(i))
 
         def finish(u):
+            kind, i = order[u]
             row, bank_sum = done[u]
-            if u % 2 == 0:
-                finish_head(u // 2, row, bank_sum)
+            if kind == "head":
+                finish_head(i, row, bank_sum)
             elif u < softmaxes - 1:
-                finish_tail(u // 2, row, bank_sum)
+                finish_tail(i, row, bank_sum)
             else:
-                finish_last_tail(u // 2, row, bank_sum)
+                finish_last_tail(i, row, bank_sum)
 
         start(0)
         start(1)
         for u in range(softmaxes):
+            kind, i = order[u]
             minus_max = minus_row_max(banks[u])
-            done[u] = exponentials(banks[u], minus_max)
+            done[u] = exponentials(banks[u], minus_max, i * ROW + (0 if kind == "head" else HEAD_TOKENS))
             if u >= 1:
                 finish(u - 1)
             if u + 2 < softmaxes:
                 start(u + 2)
 
-        ct = psum.tile([P, P], F32, tag="bank")
-        nc.tensor.transpose(ct[:], clusters[:], ident_f32[:])
-        nc.vector.tensor_copy(out=clusters_t[:], in_=ct[:])
-        nc.sync.dma_start(out=other_cluster, in_=clusters_t[TILES : 2 * TILES, :])
+        nc.sync.dma_start(out=other_cluster, in_=clusters[:, TILES : 2 * TILES])
 
         finish(softmaxes - 1)

@@ -29,9 +29,9 @@ HEAD_TOKENS = VOCAB - 2
 ROW = HEAD_TOKENS + VOCAB
 ALIGN = 8
 
+SLOTS = (0, 1, 2, 4, 5, 6, 3, 7)
+SETS = ("even", "odd")
 HEAD_PLANE = (0, 4)
-TAIL_PLANE = 8
-PROJ_PLANE = 12
 
 FLOPS = 2 * TOKENS * (D * VOCAB + D * H + H * VOCAB)
 
@@ -55,9 +55,10 @@ def tile_adaptiveinputsoftmax_pa_kernel(
 
     with ExitStack() as ctx:
         keep = ctx.enter_context(tc.tile_pool(name="keep", bufs=1))
-        stage = ctx.enter_context(tc.tile_pool(name="stage", bufs=3))
-        small = ctx.enter_context(tc.tile_pool(name="small", bufs=4))
-        psum = ctx.enter_context(tc.psum_pool(name="psum", bufs=8))
+        stage = ctx.enter_context(tc.tile_pool(name="stage", bufs=4))
+        small = ctx.enter_context(tc.tile_pool(name="small", bufs=6))
+        psum = ctx.enter_context(tc.psum_pool(name="psum", bufs=4))
+        ctx.enter_context(tc.manual_schedule())
 
         x_sb = keep.tile([P, TILES, D], BF16)
         x_codes = keep.tile([P, TILES * X_PASSES * P], U32, align_bytes=64)
@@ -65,45 +66,54 @@ def tile_adaptiveinputsoftmax_pa_kernel(
         h_codes = keep.tile([P, TILES * P], U32, align_bytes=64)
         h_scales = keep.tile([P, TILES * P], U8, align_bytes=64)
         head_w = keep.tile([P, X_PASSES, VOCAB], U32, align_bytes=64)
-        proj_w = keep.tile([P, X_PASSES, H], U32, align_bytes=64)
+        proj_raw = keep.tile([P, X_PASSES, H], U32, align_bytes=64)
+        proj_raw_scales = keep.tile([P, X_PASSES * H], U8, align_bytes=64)
+        proj_w = keep.tile([P, X_PASSES, PACK, P], U32, align_bytes=64)
+        proj_scales = keep.tile([P, X_PASSES, PACK, P], U8, align_bytes=64)
         tail_w = keep.tile([P, VOCAB], U32, align_bytes=64)
-        planes = keep.tile([P, VOCAB], U8, align_bytes=64)
+        head_planes = keep.tile([P, VOCAB], U8, align_bytes=64)
+        tail_plane = keep.tile([P, VOCAB], U8, align_bytes=64)
         ident_f32 = keep.tile([P, P], F32)
-        ident_bf16 = keep.tile([P, P], BF16)
         clusters = keep.tile([P, 2 * TILES], F32)
         out_sb = keep.tile([P, TILES * ROW], F32)
 
-        nc.vector.memset(planes[:].bitcast(I32), 0)
-
-        for i in range(TILES):
-            nc.scalar.dma_start(out=x_sb[:, i, :], in_=x_rows[:, i, :])
+        nc.vector.memset(proj_raw_scales[:].bitcast(I32), 0)
+        nc.vector.memset(head_planes[:].bitcast(I32), 0)
+        nc.vector.memset(tail_plane[:].bitcast(I32), 0)
+        make_identity(nc, ident_f32[:])
+        zero = small.tile([P, 1], F32)
+        one = small.tile([P, 1], F32)
+        nc.vector.memset(zero[:], 0.0)
+        nc.scalar.activation(out=one[:], in_=zero[:], func=ACT.Exp)
 
         for q in range(4):
             nc.sync.dma_start(
-                out=planes[32 * q + PROJ_PLANE : 32 * q + PROJ_PLANE + 4, 0 : X_PASSES * H]
+                out=proj_raw_scales[32 * q : 32 * q + 4, :]
                 .bitcast(I32)
                 .rearrange("r (g n) -> r g n", g=X_PASSES),
                 in_=tail_proj_0_scales[:, 4 * q : 4 * q + 4, :].bitcast(I32).rearrange("g r n -> r g n"),
             )
-        for q in range(4):
-            nc.sync.dma_start(
-                out=planes[32 * q + HEAD_PLANE[0] : 32 * q + HEAD_PLANE[0] + 8, :].bitcast(I32),
-                in_=head_weight_scales[:, 4 * q : 4 * q + 4, :].bitcast(I32),
-            )
-        for q in range(4):
-            nc.sync.dma_start(
-                out=planes[32 * q + TAIL_PLANE : 32 * q + TAIL_PLANE + 4, :].bitcast(I32),
-                in_=tail_w_0_scales[0, 4 * q : 4 * q + 4, :].bitcast(I32),
-            )
         nc.sync.dma_start(
-            out=proj_w[:].bitcast(I32),
+            out=proj_raw[:].bitcast(I32),
             in_=tail_proj_0_words.rearrange("g p n t -> p g (n t)").bitcast(I32),
         )
+        for i in SLOTS:
+            nc.sync.dma_start(out=x_sb[:, i, :], in_=x_rows[:, i, :])
+        for q in range(4):
+            nc.sync.dma_start(
+                out=head_planes[32 * q + HEAD_PLANE[0] : 32 * q + HEAD_PLANE[0] + 8, :].bitcast(I32),
+                in_=head_weight_scales[:, 4 * q : 4 * q + 4, :].bitcast(I32),
+            )
         head_words = head_weight_words.rearrange("g p n t -> p g (n t)")
         for c in range(ROW_BANKS):
             nc.sync.dma_start(
                 out=head_w[:, :, c * BANK : (c + 1) * BANK].bitcast(I32),
                 in_=head_words[:, :, c * BANK * PACK : (c + 1) * BANK * PACK].bitcast(I32),
+            )
+        for q in range(4):
+            nc.sync.dma_start(
+                out=tail_plane[32 * q : 32 * q + 4, :].bitcast(I32),
+                in_=tail_w_0_scales[0, 4 * q : 4 * q + 4, :].bitcast(I32),
             )
         tail_words = tail_w_0_words[0].rearrange("p n t -> p (n t)")
         for c in range(ROW_BANKS):
@@ -112,25 +122,19 @@ def tile_adaptiveinputsoftmax_pa_kernel(
                 in_=tail_words[:, c * BANK * PACK : (c + 1) * BANK * PACK].bitcast(I32),
             )
 
-        make_identity(nc, ident_f32[:])
-        make_identity(nc, ident_bf16[:])
-
-        zero = small.tile([P, 1], F32)
-        one = small.tile([P, 1], F32)
-        nc.vector.memset(zero[:], 0.0)
-        nc.scalar.activation(out=one[:], in_=zero[:], func=ACT.Exp)
-
         def transpose_x(i):
-            words = x_sb[:, i, :].bitcast(F32)
+            words = x_sb[:, SLOTS[i], :].bitcast(F32)
             half = K_PASS // 2
-            xt = psum.tile([P, X_PASSES, 2, P], F32, tag="bank")
+            xt = psum.tile([P, X_PASSES, 2, P], F32, tag=SETS[i // 4], name="xt")
             for g in range(X_PASSES):
                 for u in range(2):
                     nc.tensor.transpose(
                         xt[:, g, u, :], words[:, g * half + u : (g + 1) * half : 2], ident_f32[:]
                     )
+            return xt
+
+        def group_x(i, xt, copy):
             grouped = stage.tile([P, D], BF16, align_bytes=64, tag="x_grouped")
-            copy = nc.vector.tensor_copy if i % 2 == 0 else nc.scalar.copy
             copy(
                 out=grouped[:].bitcast(F32).rearrange("p (g r u) -> p g r u", g=X_PASSES, u=2),
                 in_=xt[:].rearrange("p g u r -> p g r u"),
@@ -147,28 +151,35 @@ def tile_adaptiveinputsoftmax_pa_kernel(
             cols = slice((i * X_PASSES + g) * P, (i * X_PASSES + g + 1) * P)
             return x_codes[:, cols], x_scales[:, cols]
 
-        def project(i, h_pair):
-            h_ps = psum.tile([P, H], F32, tag="bank")
-            for g in range(X_PASSES):
-                codes, scales = x_pass(i, g)
-                nc.tensor.matmul_mx(
-                    out=h_ps[:],
-                    lhsT=codes.bitcast(FP8X4),
-                    lhsT_scale=scales,
-                    rhs=proj_w[:, g, :].bitcast(FP8X4),
-                    rhs_scale=planes[PROJ_PLANE:P, g * H : (g + 1) * H],
-                    start=(g == 0),
-                    stop=(g == X_PASSES - 1),
-                )
-            nc.scalar.copy(out=h_pair[:, i % 2, :, :], in_=h_ps[:].rearrange("p (q t) -> p t q", t=PACK))
+        def sort_proj_columns():
+            nc.vector.tensor_copy(
+                out=proj_w[:].bitcast(I32),
+                in_=proj_raw[:].bitcast(I32).rearrange("p g (m t) -> p g t m", t=PACK),
+            )
+            by_t = proj_raw_scales[:].rearrange("p (g m t) -> p t g m", g=X_PASSES, t=PACK)
+            for t in range(PACK):
+                nc.vector.tensor_copy(out=proj_scales[:, :, t, :], in_=by_t[:, t, :, :])
 
-        def transpose_h(j, h_pair):
-            ht = psum.tile([P, 2, PACK, P], BF16, tag="bank")
-            for a in range(2):
-                for t in range(PACK):
-                    nc.tensor.transpose(ht[:, a, t, :], h_pair[:, a, t, :], ident_bf16[:])
-            grouped = stage.tile([P, 2, P, PACK], BF16, align_bytes=64, tag="h_grouped")
-            nc.scalar.copy(out=grouped[:], in_=ht[:].rearrange("p a t r -> p a r t"))
+        def project(i):
+            h_ps = psum.tile([P, PACK, P], F32, tag=SETS[1], name="h_ps")
+            for t in range(PACK):
+                for g in range(X_PASSES):
+                    codes, scales = x_pass(i, g)
+                    nc.tensor.matmul_mx(
+                        out=h_ps[:, t, :],
+                        lhsT=proj_w[:, g, t, :].bitcast(FP8X4),
+                        lhsT_scale=proj_scales[:, g, t, :],
+                        rhs=codes.bitcast(FP8X4),
+                        rhs_scale=scales,
+                        start=(g == 0),
+                        stop=(g == X_PASSES - 1),
+                    )
+            return h_ps
+
+        def round_h(i, h_ps, grouped, copy):
+            copy(out=grouped[:, i % 2, :, :], in_=h_ps[:].rearrange("p t r -> p r t"))
+
+        def quantise_h(j, grouped):
             cols = slice(2 * j * P, 2 * (j + 1) * P)
             nc.vector.quantize_mx(
                 out=h_codes[:, cols].bitcast(FP8X4),
@@ -176,60 +187,37 @@ def tile_adaptiveinputsoftmax_pa_kernel(
                 in_=grouped[:].rearrange("p a r t -> p (a r t)"),
             )
 
-        def head_passes(i):
-            return [
-                x_pass(i, g) + (head_w[:, g, :], planes[HEAD_PLANE[g] : P, :]) for g in range(X_PASSES)
-            ]
-
-        def tail_passes(i):
+        def passes_of(kind, i):
+            if kind == "head":
+                return [
+                    x_pass(i, g) + (head_w[:, g, :], head_planes[HEAD_PLANE[g] : P, :]) for g in range(X_PASSES)
+                ]
             cols = slice(i * P, (i + 1) * P)
-            return [(h_codes[:, cols], h_scales[:, cols], tail_w[:], planes[TAIL_PLANE:P, :])]
+            return [(h_codes[:, cols], h_scales[:, cols], tail_w[:], tail_plane[:])]
 
-        def logits(passes):
-            banks = []
-            for c in range(ROW_BANKS):
-                cols = slice(c * BANK, (c + 1) * BANK)
-                bank = psum.tile([P, BANK], F32, tag="bank")
-                for k, (codes, scales, w_words, w_scales) in enumerate(passes):
-                    nc.tensor.matmul_mx(
-                        out=bank[:],
-                        lhsT=codes.bitcast(FP8X4),
-                        lhsT_scale=scales,
-                        rhs=w_words[:, cols].bitcast(FP8X4),
-                        rhs_scale=w_scales[:, cols],
-                        start=(k == 0),
-                        stop=(k == len(passes) - 1),
-                    )
-                banks.append(bank)
-            return banks
-
-        def minus_row_max(banks):
-            bank_max = small.tile([P, ROW_BANKS], F32)
-            for c, bank in enumerate(banks):
-                nc.vector.reduce_max(out=bank_max[:, c : c + 1], in_=bank[:], axis=AXIS.X)
-            minus_max = small.tile([P, 1], F32)
-            nc.vector.tensor_reduce(out=minus_max[:], in_=bank_max[:], axis=AXIS.X, op=ALU.max, negate=True)
-            return minus_max
-
-        def exponentials(banks, minus_max, first_col):
-            row = out_sb[:, first_col : first_col + VOCAB]
-            bank_sum = small.tile([P, ROW_BANKS], F32)
-            for c, bank in enumerate(banks):
-                nc.scalar.activation(
-                    out=row[:, c * BANK : (c + 1) * BANK],
-                    in_=bank[:],
-                    func=ACT.Exp,
-                    bias=minus_max[:],
-                    accum_out=bank_sum[:, c : c + 1],
+        def logits_bank(passes, c, bank_set):
+            cols = slice(c * BANK, (c + 1) * BANK)
+            bank = psum.tile([P, BANK], F32, tag=bank_set, name="bank")
+            for k, (codes, scales, w_words, w_scales) in enumerate(passes):
+                nc.tensor.matmul_mx(
+                    out=bank[:],
+                    lhsT=codes.bitcast(FP8X4),
+                    lhsT_scale=scales,
+                    rhs=w_words[:, cols].bitcast(FP8X4),
+                    rhs_scale=w_scales[:, cols],
+                    start=(k == 0),
+                    stop=(k == len(passes) - 1),
                 )
-            return row, bank_sum
+            return bank
 
-        def one_over_sum(bank_sum):
-            total = small.tile([P, 1], F32)
-            nc.vector.reduce_sum(out=total[:], in_=bank_sum[:], axis=AXIS.X)
-            inverse = small.tile([P, 1], F32)
-            nc.vector.reciprocal(out=inverse[:], in_=total[:])
-            return inverse
+        def exponential(bank, c, minus_max, first_col, bank_sum):
+            nc.scalar.activation(
+                out=out_sb[:, first_col + c * BANK : first_col + (c + 1) * BANK],
+                in_=bank[:],
+                func=ACT.Exp,
+                bias=minus_max[:],
+                accum_out=bank_sum[:, c : c + 1],
+            )
 
         def down(col):
             return col // ALIGN * ALIGN
@@ -240,94 +228,170 @@ def tile_adaptiveinputsoftmax_pa_kernel(
         def store(lo, hi):
             nc.sync.dma_start(out=probs[:, lo:hi], in_=out_sb[:, lo:hi])
 
-        def finish_head(i, row, bank_sum):
-            inverse = one_over_sum(bank_sum)
-            nc.scalar.activation(
-                out=clusters[:, i : 2 * TILES : TILES],
-                in_=row[:, HEAD_TOKENS:VOCAB],
-                func=ACT.Copy,
-                scale=inverse[:],
-            )
-            nc.gpsimd.tensor_scalar(
-                out=row[:, 0:HEAD_TOKENS],
-                in0=row[:, 0:HEAD_TOKENS],
-                scalar1=inverse[:],
-                scalar2=0.0,
-                op0=ALU.mult,
-                op1=ALU.add,
-            )
-            store(up(i * ROW), down(i * ROW + HEAD_TOKENS))
-
-        def finish_tail(i, row, bank_sum):
-            inverse = one_over_sum(bank_sum)
-            nc.gpsimd.tensor_scalar(
-                out=row,
-                in0=row,
-                scalar1=inverse[:],
-                scalar2=clusters[:, i : i + 1],
-                op0=ALU.mult,
-                op1=ALU.mult,
-            )
-            store(down(i * ROW + HEAD_TOKENS), up((i + 1) * ROW))
-
-        def finish_last_tail(i, row, bank_sum):
-            inverse = one_over_sum(bank_sum)
-            factor = small.tile([P, 1], F32)
-            nc.scalar.activation(out=factor[:], in_=inverse[:], func=ACT.Copy, scale=clusters[:, i : i + 1])
-            for half in range(2):
-                lo = half * VOCAB // 2
-                hi = lo + VOCAB // 2
-                nc.scalar.activation(out=row[:, lo:hi], in_=row[:, lo:hi], func=ACT.Copy, scale=factor[:])
-                store(i * ROW + HEAD_TOKENS + lo, i * ROW + HEAD_TOKENS + hi)
-
-        x_grouped = {}
-        for i in range(TILES):
-            x_grouped[i] = transpose_x(i)
-            if i >= 1:
-                quantise_x(i - 1, x_grouped[i - 1])
-        quantise_x(TILES - 1, x_grouped[TILES - 1])
-
-        h_pairs = {}
-        for i in range(TILES):
-            if i % 2 == 0:
-                h_pairs[i // 2] = stage.tile([P, 2, PACK, P], BF16, tag="h_pair", bufs=TILES // 2, name="h_pair")
-            project(i, h_pairs[i // 2])
-        for j in range(TILES // 2):
-            transpose_h(j, h_pairs[j])
-
         order = [("head", 0)]
         for i in range(TILES - 1):
             order.extend([("head", i + 1), ("tail", i)])
         order.append(("tail", TILES - 1))
         softmaxes = len(order)
         banks = {}
-        done = {}
+        minus_max = {}
+        sums = {}
+        inverse = {}
 
-        def start(u):
+        def first_col(u):
             kind, i = order[u]
-            banks[u] = logits(head_passes(i) if kind == "head" else tail_passes(i))
+            return SLOTS[i] * ROW + (0 if kind == "head" else HEAD_TOKENS)
 
-        def finish(u):
+        def width(u):
+            return HEAD_TOKENS if order[u][0] == "head" else VOCAB
+
+        def border(col, u):
+            if col % ALIGN == 0:
+                return col
+            other = [v for v in range(softmaxes) if v != u and col in (first_col(v), first_col(v) + width(v))][0]
+            mine = u > other
+            starts_here = col == first_col(u)
+            return down(col) if mine == starts_here else up(col)
+
+        def store_rows(u):
+            store(border(first_col(u), u), border(first_col(u) + width(u), u))
+
+        def fill(u, c):
+            banks.setdefault(u, []).append(logits_bank(passes_of(*order[u]), c, SETS[u % 2]))
+
+        def scale_rows(u):
             kind, i = order[u]
-            row, bank_sum = done[u]
+            lo = first_col(u)
             if kind == "head":
-                finish_head(i, row, bank_sum)
-            elif u < softmaxes - 1:
-                finish_tail(i, row, bank_sum)
+                nc.gpsimd.tensor_scalar(
+                    out=out_sb[:, lo : lo + HEAD_TOKENS],
+                    in0=out_sb[:, lo : lo + HEAD_TOKENS],
+                    scalar1=inverse[u][:],
+                    scalar2=0.0,
+                    op0=ALU.mult,
+                    op1=ALU.add,
+                )
+                store_rows(u)
             else:
-                finish_last_tail(i, row, bank_sum)
+                nc.gpsimd.tensor_scalar(
+                    out=out_sb[:, lo : lo + VOCAB],
+                    in0=out_sb[:, lo : lo + VOCAB],
+                    scalar1=inverse[u][:],
+                    scalar2=clusters[:, SLOTS[i] : SLOTS[i] + 1],
+                    op0=ALU.mult,
+                    op1=ALU.mult,
+                )
+                store_rows(u)
 
-        start(0)
-        start(1)
-        for u in range(softmaxes):
+        def scale_piece_on_vector(u, c):
             kind, i = order[u]
-            minus_max = minus_row_max(banks[u])
-            done[u] = exponentials(banks[u], minus_max, i * ROW + (0 if kind == "head" else HEAD_TOKENS))
+            lo = first_col(u) + c * BANK
+            nc.vector.tensor_scalar(
+                out=out_sb[:, lo : lo + BANK],
+                in0=out_sb[:, lo : lo + BANK],
+                scalar1=inverse[u][:],
+                scalar2=clusters[:, SLOTS[i] : SLOTS[i] + 1],
+                op0=ALU.mult,
+                op1=ALU.mult,
+            )
+            store(lo, lo + BANK)
+
+        def cluster_probs(u):
+            kind, i = order[u]
+            lo = first_col(u)
+            nc.scalar.activation(
+                out=clusters[:, SLOTS[i] : 2 * TILES : TILES],
+                in_=out_sb[:, lo + HEAD_TOKENS : lo + VOCAB],
+                func=ACT.Copy,
+                scale=inverse[u][:],
+            )
+
+        def bank_maximum(u, c):
+            if c == 0:
+                bank_max[u] = small.tile([P, ROW_BANKS], F32, tag="bank_max", name="bank_max")
+            nc.vector.reduce_max(out=bank_max[u][:, c : c + 1], in_=banks[u][c][:], axis=AXIS.X)
+
+        def row_maximum(u):
+            minus_max[u] = small.tile([P, 1], F32, tag="minus_max", name="minus_max")
+            nc.vector.tensor_reduce(
+                out=minus_max[u][:], in_=bank_max[u][:], axis=AXIS.X, op=ALU.max, negate=True
+            )
+
+        def row_sum(u):
+            totals[u] = small.tile([P, 1], F32, tag="total", name="total")
+            nc.vector.reduce_sum(out=totals[u][:], in_=sums[u][:], axis=AXIS.X)
+
+        def invert_sum(u):
+            inverse[u] = small.tile([P, 1], F32, tag="inverse", name="inverse")
+            nc.vector.reciprocal(out=inverse[u][:], in_=totals[u][:])
+
+        bank_max = {}
+        totals = {}
+        sort_proj_columns()
+        x_grouped = {}
+        for i in range(TILES):
+            x_grouped[i] = group_x(i, transpose_x(i), nc.scalar.copy)
+            if i >= 1:
+                quantise_x(i - 1, x_grouped[i - 1])
+        quantise_x(TILES - 1, x_grouped[TILES - 1])
+
+        h_grouped = {}
+
+        def make_h(i, copy):
+            if i % 2 == 0:
+                h_grouped[i // 2] = stage.tile([P, 2, P, PACK], BF16, align_bytes=64, tag="h_grouped", name="h_grouped")
+            round_h(i, project(i), h_grouped[i // 2], copy)
+
+        for i in range(TILES):
+            make_h(i, nc.scalar.copy)
+            if i % 2 == 0 and i >= 2:
+                quantise_h(i // 2 - 1, h_grouped[i // 2 - 1])
+        quantise_h(TILES // 2 - 1, h_grouped[TILES // 2 - 1])
+        for u in range(2):
+            for c in range(ROW_BANKS):
+                fill(u, c)
+        for c in range(ROW_BANKS):
+            bank_maximum(0, c)
+        row_maximum(0)
+        bank_maximum(1, 0)
+        for u in range(softmaxes):
+            if u >= 2 and order[u - 2][0] == "head":
+                cluster_probs(u - 2)
+            if u == softmaxes - 1:
+                nc.sync.dma_start(out=other_cluster, in_=clusters[:, TILES : 2 * TILES])
+            sums[u] = small.tile([P, ROW_BANKS], F32, tag="sums", name="sums")
+            for c in range(ROW_BANKS):
+                exponential(banks[u][c], c, minus_max[u], first_col(u), sums[u])
+                if u + 2 < softmaxes:
+                    fill(u + 2, c)
+            if u + 1 < softmaxes:
+                bank_maximum(u + 1, 1)
             if u >= 1:
-                finish(u - 1)
+                row_sum(u - 1)
+            if u + 1 < softmaxes:
+                bank_maximum(u + 1, 2)
+            if u >= 1:
+                invert_sum(u - 1)
+            if u + 1 < softmaxes:
+                bank_maximum(u + 1, 3)
             if u + 2 < softmaxes:
-                start(u + 2)
+                bank_maximum(u + 2, 0)
+            if u + 1 < softmaxes:
+                row_maximum(u + 1)
+            if 1 <= u < softmaxes - 1:
+                scale_rows(u - 1)
 
-        nc.sync.dma_start(out=other_cluster, in_=clusters[:, TILES : 2 * TILES])
-
-        finish(softmaxes - 1)
+        u = softmaxes - 2
+        for c in range(ROW_BANKS):
+            scale_piece_on_vector(u, c)
+        u = softmaxes - 1
+        row_sum(u)
+        invert_sum(u)
+        i = SLOTS[order[u][1]]
+        factor = small.tile([P, 1], F32)
+        nc.scalar.activation(out=factor[:], in_=inverse[u][:], func=ACT.Copy, scale=clusters[:, i : i + 1])
+        for c in (0, 1, 2):
+            scale_piece_on_vector(u, c)
+        lo = first_col(u) + 3 * BANK
+        nc.scalar.activation(out=out_sb[:, lo : lo + BANK], in_=out_sb[:, lo : lo + BANK], func=ACT.Copy, scale=factor[:])
+        nc.scalar.dma_start(out=probs[:, lo : lo + BANK], in_=out_sb[:, lo : lo + BANK])

@@ -30,6 +30,7 @@ ROW = HEAD_TOKENS + VOCAB
 ALIGN = 8
 
 SLOTS = (0, 1, 2, 4, 5, 6, 3, 7)
+WARM_UP = 14
 SETS = ("even", "odd")
 HEAD_PLANE = (0, 4)
 
@@ -77,6 +78,8 @@ def tile_adaptiveinputsoftmax_pa_kernel(
         clusters = keep.tile([P, 2 * TILES], F32)
         out_sb = keep.tile([P, TILES * ROW], F32)
 
+        warm = keep.tile([P, BANK], BF16)
+        nc.vector.memset(warm[:], 0.0)
         nc.vector.memset(proj_raw_scales[:].bitcast(I32), 0)
         nc.vector.memset(head_planes[:].bitcast(I32), 0)
         nc.vector.memset(tail_plane[:].bitcast(I32), 0)
@@ -327,14 +330,11 @@ def tile_adaptiveinputsoftmax_pa_kernel(
 
         bank_max = {}
         totals = {}
+        idle = psum.tile([P, BANK], F32, tag=SETS[1], name="idle")
+        for k in range(WARM_UP):
+            nc.tensor.matmul(out=idle[:], lhsT=warm[:, 0:P], rhs=warm[:], start=True, stop=True)
         sort_proj_columns()
         x_grouped = {}
-        for i in range(TILES):
-            x_grouped[i] = group_x(i, transpose_x(i), nc.scalar.copy)
-            if i >= 1:
-                quantise_x(i - 1, x_grouped[i - 1])
-        quantise_x(TILES - 1, x_grouped[TILES - 1])
-
         h_grouped = {}
 
         def make_h(i, copy):
@@ -342,9 +342,23 @@ def tile_adaptiveinputsoftmax_pa_kernel(
                 h_grouped[i // 2] = stage.tile([P, 2, P, PACK], BF16, align_bytes=64, tag="h_grouped", name="h_grouped")
             round_h(i, project(i), h_grouped[i // 2], copy)
 
-        for i in range(TILES):
+        def prepare_x(i):
+            x_grouped[i] = group_x(i, transpose_x(i), nc.scalar.copy)
+            if i >= 1:
+                quantise_x(i - 1, x_grouped[i - 1])
+
+        for i in range(4):
+            prepare_x(i)
+        make_h(0, nc.scalar.copy)
+        make_h(1, nc.scalar.copy)
+        for i in range(4, TILES):
+            prepare_x(i)
+            if i == 4:
+                quantise_h(0, h_grouped[0])
+        quantise_x(TILES - 1, x_grouped[TILES - 1])
+        for i in range(2, TILES):
             make_h(i, nc.scalar.copy)
-            if i % 2 == 0 and i >= 2:
+            if i % 2 == 0 and i >= 4:
                 quantise_h(i // 2 - 1, h_grouped[i // 2 - 1])
         quantise_h(TILES // 2 - 1, h_grouped[TILES // 2 - 1])
         for u in range(2):

@@ -30,7 +30,7 @@ ROW = HEAD_TOKENS + VOCAB
 ALIGN = 8
 
 SLOTS = (0, 1, 2, 4, 5, 6, 3, 7)
-WARM_UP = 14
+WARM_UP = 10
 SETS = ("even", "odd")
 HEAD_PLANE = (0, 4)
 
@@ -89,6 +89,13 @@ def tile_adaptiveinputsoftmax_pa_kernel(
         nc.vector.memset(zero[:], 0.0)
         nc.scalar.activation(out=one[:], in_=zero[:], func=ACT.Exp)
 
+        def load_x(i):
+            nc.sync.dma_start(out=x_sb[:, SLOTS[i], :], in_=x_rows[:, SLOTS[i], :])
+
+        nc.sync.dma_start(
+            out=proj_raw[:].bitcast(I32),
+            in_=tail_proj_0_words.rearrange("g p n t -> p g (n t)").bitcast(I32),
+        )
         for q in range(4):
             nc.sync.dma_start(
                 out=proj_raw_scales[32 * q : 32 * q + 4, :]
@@ -96,12 +103,8 @@ def tile_adaptiveinputsoftmax_pa_kernel(
                 .rearrange("r (g n) -> r g n", g=X_PASSES),
                 in_=tail_proj_0_scales[:, 4 * q : 4 * q + 4, :].bitcast(I32).rearrange("g r n -> r g n"),
             )
-        nc.sync.dma_start(
-            out=proj_raw[:].bitcast(I32),
-            in_=tail_proj_0_words.rearrange("g p n t -> p g (n t)").bitcast(I32),
-        )
-        for i in SLOTS:
-            nc.sync.dma_start(out=x_sb[:, i, :], in_=x_rows[:, i, :])
+        for i in range(TILES):
+            load_x(i)
         for q in range(4):
             nc.sync.dma_start(
                 out=head_planes[32 * q + HEAD_PLANE[0] : 32 * q + HEAD_PLANE[0] + 8, :].bitcast(I32),
@@ -262,42 +265,40 @@ def tile_adaptiveinputsoftmax_pa_kernel(
         def fill(u, c):
             banks.setdefault(u, []).append(logits_bank(passes_of(*order[u]), c, SETS[u % 2]))
 
-        def scale_rows(u):
+        def scale_rows(u, pieces=1):
             kind, i = order[u]
-            lo = first_col(u)
-            if kind == "head":
+            first, last = first_col(u), first_col(u) + width(u)
+            cuts = [first] + [down(first + k * width(u) // pieces) for k in range(1, pieces)] + [last]
+            for lo, hi in zip(cuts[:-1], cuts[1:]):
                 nc.gpsimd.tensor_scalar(
-                    out=out_sb[:, lo : lo + HEAD_TOKENS],
-                    in0=out_sb[:, lo : lo + HEAD_TOKENS],
+                    out=out_sb[:, lo:hi],
+                    in0=out_sb[:, lo:hi],
                     scalar1=inverse[u][:],
-                    scalar2=0.0,
+                    scalar2=0.0 if kind == "head" else clusters[:, SLOTS[i] : SLOTS[i] + 1],
                     op0=ALU.mult,
-                    op1=ALU.add,
+                    op1=ALU.add if kind == "head" else ALU.mult,
                 )
-                store_rows(u)
-            else:
-                nc.gpsimd.tensor_scalar(
-                    out=out_sb[:, lo : lo + VOCAB],
-                    in0=out_sb[:, lo : lo + VOCAB],
-                    scalar1=inverse[u][:],
-                    scalar2=clusters[:, SLOTS[i] : SLOTS[i] + 1],
-                    op0=ALU.mult,
-                    op1=ALU.mult,
-                )
-                store_rows(u)
+                store(border(lo, u) if lo == first else lo, border(hi, u) if hi == last else hi)
 
-        def scale_piece_on_vector(u, c):
+        def scale_piece_on_vector(u, c, cols=BANK):
             kind, i = order[u]
-            lo = first_col(u) + c * BANK
+            lo = up(first_col(u)) if c == 0 else down(first_col(u) + c * cols)
+            hi = down(first_col(u) + (c + 1) * cols) if (c + 1) * cols < VOCAB else first_col(u) + width(u)
             nc.vector.tensor_scalar(
-                out=out_sb[:, lo : lo + BANK],
-                in0=out_sb[:, lo : lo + BANK],
+                out=out_sb[:, lo:hi],
+                in0=out_sb[:, lo:hi],
                 scalar1=inverse[u][:],
-                scalar2=clusters[:, SLOTS[i] : SLOTS[i] + 1],
+                scalar2=1.0 if kind == "head" else clusters[:, SLOTS[i] : SLOTS[i] + 1],
                 op0=ALU.mult,
                 op1=ALU.mult,
             )
-            store(lo, lo + BANK)
+            store(border(first_col(u), u) if c == 0 else lo, hi)
+
+        def scale_sliver_on_scalar(u):
+            lo = first_col(u)
+            nc.scalar.activation(
+                out=out_sb[:, lo : up(lo)], in_=out_sb[:, lo : up(lo)], func=ACT.Copy, scale=inverse[u][:]
+            )
 
         def cluster_probs(u):
             kind, i = order[u]
@@ -356,17 +357,26 @@ def tile_adaptiveinputsoftmax_pa_kernel(
             if i == 4:
                 quantise_h(0, h_grouped[0])
         quantise_x(TILES - 1, x_grouped[TILES - 1])
-        for i in range(2, TILES):
-            make_h(i, nc.scalar.copy)
-            if i % 2 == 0 and i >= 4:
-                quantise_h(i // 2 - 1, h_grouped[i // 2 - 1])
-        quantise_h(TILES // 2 - 1, h_grouped[TILES // 2 - 1])
-        for u in range(2):
-            for c in range(ROW_BANKS):
-                fill(u, c)
-        for c in range(ROW_BANKS):
-            bank_maximum(0, c)
+        make_h(2, nc.scalar.copy)
+        make_h(3, nc.scalar.copy)
+        make_h(4, nc.scalar.copy)
+        quantise_h(1, h_grouped[1])
+        make_h(5, nc.scalar.copy)
+        fill(0, 0)
+        bank_maximum(0, 0)
+        fill(0, 1)
+        bank_maximum(0, 1)
+        make_h(6, nc.scalar.copy)
+        quantise_h(2, h_grouped[2])
+        fill(0, 2)
+        bank_maximum(0, 2)
+        make_h(7, nc.scalar.copy)
+        fill(0, 3)
+        bank_maximum(0, 3)
         row_maximum(0)
+        for c in range(ROW_BANKS):
+            fill(1, c)
+        quantise_h(3, h_grouped[3])
         bank_maximum(1, 0)
         for u in range(softmaxes):
             if u >= 2 and order[u - 2][0] == "head":
@@ -388,16 +398,20 @@ def tile_adaptiveinputsoftmax_pa_kernel(
                 invert_sum(u - 1)
             if u + 1 < softmaxes:
                 bank_maximum(u + 1, 3)
+            if u == 0:
+                row_maximum(u + 1)
             if u + 2 < softmaxes:
                 bank_maximum(u + 2, 0)
-            if u + 1 < softmaxes:
-                row_maximum(u + 1)
             if 1 <= u < softmaxes - 1:
-                scale_rows(u - 1)
+                row_maximum(u + 1)
+            if 1 <= u < softmaxes - (3 - 1):
+                scale_rows(u - 1, 2 if u - 1 >= 10 else 1)
+            elif u >= 1:
+                if order[u - 1][0] == "head":
+                    scale_sliver_on_scalar(u - 1)
+                for c in range(VOCAB // 1024):
+                    scale_piece_on_vector(u - 1, c, 1024)
 
-        u = softmaxes - 2
-        for c in range(ROW_BANKS):
-            scale_piece_on_vector(u, c)
         u = softmaxes - 1
         row_sum(u)
         invert_sum(u)

@@ -128,15 +128,27 @@ def tile_adaptiveinputsoftmax_pa_kernel(
                 in_=tail_words[:, c * BANK * PACK : (c + 1) * BANK * PACK].bitcast(I32),
             )
 
+        x_sorted = {}
+
+        def sort_words(i):
+            words = x_sb[:, SLOTS[i], :].bitcast(F32)
+            x_sorted[i] = stage.tile([P, X_PASSES, 2, P], F32, tag="sorted_words", name="sorted_words")
+            nc.vector.tensor_copy(
+                out=x_sorted[i][:], in_=words.rearrange("p (g w u) -> p g u w", g=X_PASSES, u=2)
+            )
+
         def transpose_x(i):
+            xt = psum.tile([P, X_PASSES, 2, P], F32, tag=SETS[i // 4], name="xt")
             words = x_sb[:, SLOTS[i], :].bitcast(F32)
             half = K_PASS // 2
-            xt = psum.tile([P, X_PASSES, 2, P], F32, tag=SETS[i // 4], name="xt")
             for g in range(X_PASSES):
                 for u in range(2):
-                    nc.tensor.transpose(
-                        xt[:, g, u, :], words[:, g * half + u : (g + 1) * half : 2], ident_f32[:]
-                    )
+                    if i in x_sorted:
+                        nc.tensor.transpose(xt[:, g, u, :], x_sorted[i][:, g, u, :], ident_f32[:])
+                    else:
+                        nc.tensor.transpose(
+                            xt[:, g, u, :], words[:, g * half + u : (g + 1) * half : 2], ident_f32[:]
+                        )
             return xt
 
         def group_x(i, xt, copy):
@@ -157,11 +169,13 @@ def tile_adaptiveinputsoftmax_pa_kernel(
             cols = slice((i * X_PASSES + g) * P, (i * X_PASSES + g + 1) * P)
             return x_codes[:, cols], x_scales[:, cols]
 
-        def sort_proj_columns():
+        def sort_proj_codes():
             nc.vector.tensor_copy(
                 out=proj_w[:].bitcast(I32),
                 in_=proj_raw[:].bitcast(I32).rearrange("p g (m t) -> p g t m", t=PACK),
             )
+
+        def sort_proj_scales():
             by_t = proj_raw_scales[:].rearrange("p (g m t) -> p t g m", g=X_PASSES, t=PACK)
             for t in range(PACK):
                 nc.vector.tensor_copy(out=proj_scales[:, :, t, :], in_=by_t[:, t, :, :])
@@ -334,7 +348,6 @@ def tile_adaptiveinputsoftmax_pa_kernel(
         idle = psum.tile([P, BANK], F32, tag=SETS[1], name="idle")
         for k in range(WARM_UP):
             nc.tensor.matmul(out=idle[:], lhsT=warm[:, 0:P], rhs=warm[:], start=True, stop=True)
-        sort_proj_columns()
         x_grouped = {}
         h_grouped = {}
 
@@ -343,10 +356,19 @@ def tile_adaptiveinputsoftmax_pa_kernel(
                 h_grouped[i // 2] = stage.tile([P, 2, P, PACK], BF16, align_bytes=64, tag="h_grouped", name="h_grouped")
             round_h(i, project(i), h_grouped[i // 2], copy)
 
+        AHEAD = 3
+        sort_proj_codes()
+        for i in range(AHEAD):
+            sort_words(i)
+            if i == 1:
+                sort_proj_scales()
+
         def prepare_x(i):
             x_grouped[i] = group_x(i, transpose_x(i), nc.scalar.copy)
             if i >= 1:
                 quantise_x(i - 1, x_grouped[i - 1])
+            if i + AHEAD < TILES:
+                sort_words(i + AHEAD)
 
         for i in range(4):
             prepare_x(i)

@@ -27,8 +27,8 @@ VOCAB = 2048
 ROW_BANKS = VOCAB // BANK
 HEAD_TOKENS = VOCAB - 2
 ROW = HEAD_TOKENS + VOCAB
-ALIGN = 8
 
+SPAN = 2 * VOCAB
 SLOTS = (0, 1, 2, 4, 5, 6, 3, 7)
 WARM_UP = 10
 SETS = ("even", "odd")
@@ -75,8 +75,8 @@ def tile_adaptiveinputsoftmax_pa_kernel(
         head_planes = keep.tile([P, VOCAB], U8, align_bytes=64)
         tail_plane = keep.tile([P, VOCAB], U8, align_bytes=64)
         ident_f32 = keep.tile([P, P], F32)
-        clusters = keep.tile([P, 2 * TILES], F32)
-        out_sb = keep.tile([P, TILES * ROW], F32)
+        others = keep.tile([P, TILES], F32)
+        out_sb = keep.tile([P, TILES * SPAN], F32)
 
         warm = keep.tile([P, BANK], BF16)
         nc.vector.memset(warm[:], 0.0)
@@ -239,15 +239,6 @@ def tile_adaptiveinputsoftmax_pa_kernel(
                 accum_out=bank_sum[:, c : c + 1],
             )
 
-        def down(col):
-            return col // ALIGN * ALIGN
-
-        def up(col):
-            return (col + ALIGN - 1) // ALIGN * ALIGN
-
-        def store(lo, hi):
-            nc.sync.dma_start(out=probs[:, lo:hi], in_=out_sb[:, lo:hi])
-
         order = [("head", 0)]
         for i in range(TILES - 1):
             order.extend([("head", i + 1), ("tail", i)])
@@ -260,69 +251,49 @@ def tile_adaptiveinputsoftmax_pa_kernel(
 
         def first_col(u):
             kind, i = order[u]
-            return SLOTS[i] * ROW + (0 if kind == "head" else HEAD_TOKENS)
+            return SLOTS[i] * SPAN + (0 if kind == "head" else VOCAB)
 
-        def width(u):
-            return HEAD_TOKENS if order[u][0] == "head" else VOCAB
+        def cluster_of(u):
+            kind, i = order[u]
+            col = SLOTS[i] * SPAN + HEAD_TOKENS
+            return None if kind == "head" else out_sb[:, col : col + 1]
 
-        def border(col, u):
-            if col % ALIGN == 0:
-                return col
-            other = [v for v in range(softmaxes) if v != u and col in (first_col(v), first_col(v) + width(v))][0]
-            mine = u > other
-            starts_here = col == first_col(u)
-            return down(col) if mine == starts_here else up(col)
-
-        def store_rows(u):
-            store(border(first_col(u), u), border(first_col(u) + width(u), u))
+        def store(u, lo, hi, queue=nc.sync):
+            kind, i = order[u]
+            at = SLOTS[i] * ROW + (0 if kind == "head" else HEAD_TOKENS)
+            first = first_col(u)
+            hi = min(hi, HEAD_TOKENS) if kind == "head" else hi
+            queue.dma_start(out=probs[:, at + lo : at + hi], in_=out_sb[:, first + lo : first + hi])
 
         def fill(u, c):
             banks.setdefault(u, []).append(logits_bank(passes_of(*order[u]), c, SETS[u % 2]))
 
         def scale_rows(u, pieces=1):
-            kind, i = order[u]
-            first, last = first_col(u), first_col(u) + width(u)
-            cuts = [first] + [down(first + k * width(u) // pieces) for k in range(1, pieces)] + [last]
-            for lo, hi in zip(cuts[:-1], cuts[1:]):
+            first, cols, cluster = first_col(u), VOCAB // pieces, cluster_of(u)
+            for k in range(pieces):
+                part = out_sb[:, first + k * cols : first + (k + 1) * cols]
                 nc.gpsimd.tensor_scalar(
-                    out=out_sb[:, lo:hi],
-                    in0=out_sb[:, lo:hi],
+                    out=part,
+                    in0=part,
                     scalar1=inverse[u][:],
-                    scalar2=0.0 if kind == "head" else clusters[:, SLOTS[i] : SLOTS[i] + 1],
+                    scalar2=0.0 if cluster is None else cluster,
                     op0=ALU.mult,
-                    op1=ALU.add if kind == "head" else ALU.mult,
+                    op1=ALU.add if cluster is None else ALU.mult,
                 )
-                store(border(lo, u) if lo == first else lo, border(hi, u) if hi == last else hi)
+                store(u, k * cols, (k + 1) * cols)
 
         def scale_piece_on_vector(u, c, cols=BANK):
-            kind, i = order[u]
-            lo = up(first_col(u)) if c == 0 else down(first_col(u) + c * cols)
-            hi = down(first_col(u) + (c + 1) * cols) if (c + 1) * cols < VOCAB else first_col(u) + width(u)
+            first, cluster = first_col(u), cluster_of(u)
+            part = out_sb[:, first + c * cols : first + (c + 1) * cols]
             nc.vector.tensor_scalar(
-                out=out_sb[:, lo:hi],
-                in0=out_sb[:, lo:hi],
+                out=part,
+                in0=part,
                 scalar1=inverse[u][:],
-                scalar2=1.0 if kind == "head" else clusters[:, SLOTS[i] : SLOTS[i] + 1],
+                scalar2=1.0 if cluster is None else cluster,
                 op0=ALU.mult,
                 op1=ALU.mult,
             )
-            store(border(first_col(u), u) if c == 0 else lo, hi)
-
-        def scale_sliver_on_scalar(u):
-            lo = first_col(u)
-            nc.scalar.activation(
-                out=out_sb[:, lo : up(lo)], in_=out_sb[:, lo : up(lo)], func=ACT.Copy, scale=inverse[u][:]
-            )
-
-        def cluster_probs(u):
-            kind, i = order[u]
-            lo = first_col(u)
-            nc.scalar.activation(
-                out=clusters[:, SLOTS[i] : 2 * TILES : TILES],
-                in_=out_sb[:, lo + HEAD_TOKENS : lo + VOCAB],
-                func=ACT.Copy,
-                scale=inverse[u][:],
-            )
+            store(u, c * cols, (c + 1) * cols)
 
         def bank_maximum(u, c):
             if c == 0:
@@ -401,10 +372,6 @@ def tile_adaptiveinputsoftmax_pa_kernel(
         quantise_h(3, h_grouped[3])
         bank_maximum(1, 0)
         for u in range(softmaxes):
-            if u >= 2 and order[u - 2][0] == "head":
-                cluster_probs(u - 2)
-            if u == softmaxes - 1:
-                nc.sync.dma_start(out=other_cluster, in_=clusters[:, TILES : 2 * TILES])
             sums[u] = small.tile([P, ROW_BANKS], F32, tag="sums", name="sums")
             for c in range(ROW_BANKS):
                 exponential(banks[u][c], c, minus_max[u], first_col(u), sums[u])
@@ -429,19 +396,18 @@ def tile_adaptiveinputsoftmax_pa_kernel(
             if 1 <= u < softmaxes - (3 - 1):
                 scale_rows(u - 1, 2 if u - 1 >= 10 else 1)
             elif u >= 1:
-                if order[u - 1][0] == "head":
-                    scale_sliver_on_scalar(u - 1)
                 for c in range(VOCAB // 1024):
                     scale_piece_on_vector(u - 1, c, 1024)
 
+        nc.gpsimd.tensor_copy(out=others[:], in_=out_sb[:, VOCAB - 1 : TILES * SPAN : SPAN])
         u = softmaxes - 1
         row_sum(u)
         invert_sum(u)
-        i = SLOTS[order[u][1]]
         factor = small.tile([P, 1], F32)
-        nc.scalar.activation(out=factor[:], in_=inverse[u][:], func=ACT.Copy, scale=clusters[:, i : i + 1])
+        nc.scalar.activation(out=factor[:], in_=inverse[u][:], func=ACT.Copy, scale=cluster_of(u))
         for c in (0, 1, 2):
             scale_piece_on_vector(u, c)
         lo = first_col(u) + 3 * BANK
         nc.scalar.activation(out=out_sb[:, lo : lo + BANK], in_=out_sb[:, lo : lo + BANK], func=ACT.Copy, scale=factor[:])
-        nc.scalar.dma_start(out=probs[:, lo : lo + BANK], in_=out_sb[:, lo : lo + BANK])
+        store(u, 3 * BANK, VOCAB, nc.scalar)
+        nc.sync.dma_start(out=other_cluster, in_=others[:])

@@ -180,8 +180,8 @@ def tile_adaptiveinputsoftmax_pa_kernel(
             for t in range(PACK):
                 nc.vector.tensor_copy(out=proj_scales[:, :, t, :], in_=by_t[:, t, :, :])
 
-        def project(i):
-            h_ps = psum.tile([P, PACK, P], F32, tag=SETS[1], name="h_ps")
+        def project(i, ring=1):
+            h_ps = psum.tile([P, PACK, P], F32, tag=SETS[ring], name="h_ps")
             for t in range(PACK):
                 for g in range(X_PASSES):
                     codes, scales = x_pass(i, g)
@@ -336,6 +336,9 @@ def tile_adaptiveinputsoftmax_pa_kernel(
 
         def prepare_x(i):
             x_grouped[i] = group_x(i, transpose_x(i), nc.scalar.copy)
+            if i == 1:
+                for k in range(2):
+                    nc.tensor.matmul(out=idle[:, 0:384], lhsT=warm[:, 0:P], rhs=warm[:, 0:384], start=True, stop=True)
             if i >= 1:
                 quantise_x(i - 1, x_grouped[i - 1])
             if i + AHEAD < TILES:
@@ -355,34 +358,36 @@ def tile_adaptiveinputsoftmax_pa_kernel(
         make_h(4, nc.scalar.copy)
         quantise_h(1, h_grouped[1])
         make_h(5, nc.scalar.copy)
-        fill(0, 0)
-        bank_maximum(0, 0)
-        fill(0, 1)
-        bank_maximum(0, 1)
-        make_h(6, nc.scalar.copy)
-        quantise_h(2, h_grouped[2])
-        fill(0, 2)
-        bank_maximum(0, 2)
-        make_h(7, nc.scalar.copy)
-        fill(0, 3)
-        bank_maximum(0, 3)
+        for c in range(ROW_BANKS):
+            fill(0, c)
+            bank_maximum(0, c)
         row_maximum(0)
+        quantise_h(2, h_grouped[2])
         for c in range(ROW_BANKS):
             fill(1, c)
-        quantise_h(3, h_grouped[3])
         bank_maximum(1, 0)
+        last_h = []
         for u in range(softmaxes):
             sums[u] = small.tile([P, ROW_BANKS], F32, tag="sums", name="sums")
             for c in range(ROW_BANKS):
                 exponential(banks[u][c], c, minus_max[u], first_col(u), sums[u])
-                if u + 2 < softmaxes:
-                    fill(u + 2, c)
+                if u == 0 and c < 2:
+                    last_h.append(project(6 + c, 0))
+                elif u + 2 < softmaxes:
+                    fill(u + 2, c - 2 if u == 0 else c)
+            if u == 0:
+                h_grouped[3] = stage.tile([P, 2, P, PACK], BF16, align_bytes=64, tag="h_grouped", name="h_grouped")
+                for c in range(2):
+                    round_h(6 + c, last_h[c], h_grouped[3], nc.scalar.copy)
+                    fill(2, 2 + c)
             if u + 1 < softmaxes:
                 bank_maximum(u + 1, 1)
             if u >= 1:
                 row_sum(u - 1)
             if u + 1 < softmaxes:
                 bank_maximum(u + 1, 2)
+            if u == 1:
+                quantise_h(3, h_grouped[3])
             if u >= 1:
                 invert_sum(u - 1)
             if u + 1 < softmaxes:
@@ -394,12 +399,13 @@ def tile_adaptiveinputsoftmax_pa_kernel(
             if 1 <= u < softmaxes - 1:
                 row_maximum(u + 1)
             if 1 <= u < softmaxes - (3 - 1):
-                scale_rows(u - 1, 2 if u - 1 >= 10 else 1)
+                scale_rows(u - 1, 2 if u - 1 >= 11 else 1)
             elif u >= 1:
                 for c in range(VOCAB // 1024):
                     scale_piece_on_vector(u - 1, c, 1024)
 
         nc.gpsimd.tensor_copy(out=others[:], in_=out_sb[:, VOCAB - 1 : TILES * SPAN : SPAN])
+        nc.sync.dma_start(out=other_cluster, in_=others[:])
         u = softmaxes - 1
         row_sum(u)
         invert_sum(u)
@@ -410,4 +416,3 @@ def tile_adaptiveinputsoftmax_pa_kernel(
         lo = first_col(u) + 3 * BANK
         nc.scalar.activation(out=out_sb[:, lo : lo + BANK], in_=out_sb[:, lo : lo + BANK], func=ACT.Copy, scale=factor[:])
         store(u, 3 * BANK, VOCAB, nc.scalar)
-        nc.sync.dma_start(out=other_cluster, in_=others[:])

@@ -29,7 +29,7 @@ HEAD_TOKENS = VOCAB - 2
 ROW = HEAD_TOKENS + VOCAB
 
 SPAN = 2 * VOCAB
-SLOTS = (0, 1, 2, 4, 5, 6, 3, 7)
+SLOTS = tuple(range(TILES))
 WARM_UP = 10
 SETS = ("even", "odd")
 HEAD_PLANE = (0, 4)
@@ -89,8 +89,8 @@ def tile_adaptiveinputsoftmax_pa_kernel(
         nc.vector.memset(zero[:], 0.0)
         nc.scalar.activation(out=one[:], in_=zero[:], func=ACT.Exp)
 
-        def load_x(i):
-            nc.sync.dma_start(out=x_sb[:, SLOTS[i], :], in_=x_rows[:, SLOTS[i], :])
+        def load_x(i, tiles):
+            nc.sync.dma_start(out=x_sb[:, i : i + tiles, :], in_=x_rows[:, i : i + tiles, :])
 
         nc.sync.dma_start(
             out=proj_raw[:].bitcast(I32),
@@ -103,18 +103,17 @@ def tile_adaptiveinputsoftmax_pa_kernel(
                 .rearrange("r (g n) -> r g n", g=X_PASSES),
                 in_=tail_proj_0_scales[:, 4 * q : 4 * q + 4, :].bitcast(I32).rearrange("g r n -> r g n"),
             )
-        for i in range(TILES):
-            load_x(i)
+        for i, tiles in ((0, 1), (1, 1), (2, 2), (4, 2), (6, 2)):
+            load_x(i, tiles)
         for q in range(4):
             nc.sync.dma_start(
                 out=head_planes[32 * q + HEAD_PLANE[0] : 32 * q + HEAD_PLANE[0] + 8, :].bitcast(I32),
                 in_=head_weight_scales[:, 4 * q : 4 * q + 4, :].bitcast(I32),
             )
         head_words = head_weight_words.rearrange("g p n t -> p g (n t)")
-        for c in range(ROW_BANKS):
+        for lo, hi in ((0, 2 * BANK), (2 * BANK, VOCAB)):
             nc.sync.dma_start(
-                out=head_w[:, :, c * BANK : (c + 1) * BANK].bitcast(I32),
-                in_=head_words[:, :, c * BANK * PACK : (c + 1) * BANK * PACK].bitcast(I32),
+                out=head_w[:, :, lo:hi].bitcast(I32), in_=head_words[:, :, lo * PACK : hi * PACK].bitcast(I32)
             )
         for q in range(4):
             nc.sync.dma_start(
@@ -122,11 +121,8 @@ def tile_adaptiveinputsoftmax_pa_kernel(
                 in_=tail_w_0_scales[0, 4 * q : 4 * q + 4, :].bitcast(I32),
             )
         tail_words = tail_w_0_words[0].rearrange("p n t -> p (n t)")
-        for c in range(ROW_BANKS):
-            nc.sync.dma_start(
-                out=tail_w[:, c * BANK : (c + 1) * BANK].bitcast(I32),
-                in_=tail_words[:, c * BANK * PACK : (c + 1) * BANK * PACK].bitcast(I32),
-            )
+        for lo, hi in ((0, 2 * BANK), (2 * BANK, VOCAB)):
+            nc.sync.dma_start(out=tail_w[:, lo:hi].bitcast(I32), in_=tail_words[:, lo * PACK : hi * PACK].bitcast(I32))
 
         x_sorted = {}
 

@@ -397,8 +397,7 @@ def tile_adaptiveinputsoftmax_pa_kernel(
             if 1 <= u < softmaxes - (3 - 1):
                 scale_rows(u - 1, 2 if u - 1 >= 11 else 1)
             elif u >= 1:
-                for c in range(VOCAB // 1024):
-                    scale_piece_on_vector(u - 1, c, 1024)
+                scale_piece_on_vector(u - 1, 0, VOCAB)
 
         nc.gpsimd.tensor_copy(out=others[:], in_=out_sb[:, VOCAB - 1 : TILES * SPAN : SPAN])
         nc.sync.dma_start(out=other_cluster, in_=others[:])
@@ -407,8 +406,8 @@ def tile_adaptiveinputsoftmax_pa_kernel(
         invert_sum(u)
         factor = small.tile([P, 1], F32)
         nc.scalar.activation(out=factor[:], in_=inverse[u][:], func=ACT.Copy, scale=cluster_of(u))
-        for c in (0, 1, 2):
-            scale_piece_on_vector(u, c)
+        scale_piece_on_vector(u, 0, 2 * BANK)
+        scale_piece_on_vector(u, 2)
         lo = first_col(u) + 3 * BANK
         nc.scalar.activation(out=out_sb[:, lo : lo + BANK], in_=out_sb[:, lo : lo + BANK], func=ACT.Copy, scale=factor[:])
         store(u, 3 * BANK, VOCAB, nc.scalar)

from contextlib import ExitStack

import concourse.mybir as mybir
from concourse.masks import make_identity

F32 = mybir.dt.float32
BF16 = mybir.dt.bfloat16
I32 = mybir.dt.int32
U32 = mybir.dt.uint32
U8 = mybir.dt.uint8
FP8X4 = mybir.dt.float8_e4m3fn_x4
ALU = mybir.AluOpType
ACT = mybir.ActivationFunctionType
AXIS = mybir.AxisListType

P = 128
PACK = 4
K_PASS = P * PACK
BANK = 512

TOKENS = 1024
TILES = TOKENS // P
D = 1024
X_PASSES = D // K_PASS
H = 512
VOCAB = 2048
ROW_BANKS = VOCAB // BANK
HEAD_TOKENS = VOCAB - 2
ROW = HEAD_TOKENS + VOCAB

SPAN = 2 * VOCAB
SLOTS = tuple(range(TILES))
WARM_UP = 10
SETS = ("even", "odd")
HEAD_PLANE = (0, 4)

FLOPS = 2 * TOKENS * (D * VOCAB + D * H + H * VOCAB)


def tile_adaptiveinputsoftmax_pa_kernel(
    tc,
    x,
    head_weight_words,
    head_weight_scales,
    tail_proj_0_words,
    tail_proj_0_scales,
    tail_w_0_words,
    tail_w_0_scales,
    out_0,
    out_1,
):
    nc = tc.nc
    x_rows = x.flatten_outer_dims().rearrange("(p i) d -> p i d", i=TILES)
    probs = out_0.flatten_outer_dims().rearrange("(p i) c -> p (i c)", i=TILES)
    other_cluster = out_1.rearrange("n t o -> (n t o)").rearrange("(p i) -> p i", i=TILES)

    with ExitStack() as ctx:
        keep = ctx.enter_context(tc.tile_pool(name="keep", bufs=1))
        stage = ctx.enter_context(tc.tile_pool(name="stage", bufs=4))
        small = ctx.enter_context(tc.tile_pool(name="small", bufs=6))
        psum = ctx.enter_context(tc.psum_pool(name="psum", bufs=4))
        ctx.enter_context(tc.manual_schedule())

        x_sb = keep.tile([P, TILES, D], BF16)
        x_codes = keep.tile([P, TILES * X_PASSES * P], U32, align_bytes=64)
        x_scales = keep.tile([P, TILES * X_PASSES * P], U8, align_bytes=64)
        h_codes = keep.tile([P, TILES * P], U32, align_bytes=64)
        h_scales = keep.tile([P, TILES * P], U8, align_bytes=64)
        head_w = keep.tile([P, X_PASSES, VOCAB], U32, align_bytes=64)
        proj_raw = keep.tile([P, X_PASSES, H], U32, align_bytes=64)
        proj_raw_scales = keep.tile([P, X_PASSES * H], U8, align_bytes=64)
        proj_w = keep.tile([P, X_PASSES, PACK, P], U32, align_bytes=64)
        proj_scales = keep.tile([P, X_PASSES, PACK, P], U8, align_bytes=64)
        tail_w = keep.tile([P, VOCAB], U32, align_bytes=64)
        head_planes = keep.tile([P, VOCAB], U8, align_bytes=64)
        tail_plane = keep.tile([P, VOCAB], U8, align_bytes=64)
        ident_f32 = keep.tile([P, P], F32)
        others = keep.tile([P, TILES], F32)
        out_sb = keep.tile([P, TILES * SPAN], F32)

        warm = keep.tile([P, BANK], BF16)
        nc.vector.memset(warm[:], 0.0)
        nc.vector.memset(proj_raw_scales[:].bitcast(I32), 0)
        nc.vector.memset(head_planes[:].bitcast(I32), 0)
        nc.vector.memset(tail_plane[:].bitcast(I32), 0)
        make_identity(nc, ident_f32[:])
        zero = small.tile([P, 1], F32)
        one = small.tile([P, 1], F32)
        nc.vector.memset(zero[:], 0.0)
        nc.scalar.activation(out=one[:], in_=zero[:], func=ACT.Exp)

        def load_x(i, tiles):
            nc.sync.dma_start(out=x_sb[:, i : i + tiles, :], in_=x_rows[:, i : i + tiles, :])

        nc.sync.dma_start(
            out=proj_raw[:].bitcast(I32),
            in_=tail_proj_0_words.rearrange("g p n t -> p g (n t)").bitcast(I32),
        )
        for q in range(4):
            nc.sync.dma_start(
                out=proj_raw_scales[32 * q : 32 * q + 4, :]
                .bitcast(I32)
                .rearrange("r (g n) -> r g n", g=X_PASSES),
                in_=tail_proj_0_scales[:, 4 * q : 4 * q + 4, :].bitcast(I32).rearrange("g r n -> r g n"),
            )
        for i, tiles in ((0, 1), (1, 1), (2, 2), (4, 2), (6, 2)):
            load_x(i, tiles)
        for q in range(4):
            nc.sync.dma_start(
                out=head_planes[32 * q + HEAD_PLANE[0] : 32 * q + HEAD_PLANE[0] + 8, :].bitcast(I32),
                in_=head_weight_scales[:, 4 * q : 4 * q + 4, :].bitcast(I32),
            )
        head_words = head_weight_words.rearrange("g p n t -> p g (n t)")
        for lo, hi in ((0, 2 * BANK), (2 * BANK, VOCAB)):
            nc.sync.dma_start(
                out=head_w[:, :, lo:hi].bitcast(I32), in_=head_words[:, :, lo * PACK : hi * PACK].bitcast(I32)
            )
        for q in range(4):
            nc.sync.dma_start(
                out=tail_plane[32 * q : 32 * q + 4, :].bitcast(I32),
                in_=tail_w_0_scales[0, 4 * q : 4 * q + 4, :].bitcast(I32),
            )
        tail_words = tail_w_0_words[0].rearrange("p n t -> p (n t)")
        for lo, hi in ((0, 2 * BANK), (2 * BANK, VOCAB)):
            nc.sync.dma_start(out=tail_w[:, lo:hi].bitcast(I32), in_=tail_words[:, lo * PACK : hi * PACK].bitcast(I32))

        x_sorted = {}

        def sort_words(i):
            words = x_sb[:, SLOTS[i], :].bitcast(F32)
            x_sorted[i] = stage.tile([P, X_PASSES, 2, P], F32, tag="sorted_words", name="sorted_words")
            nc.vector.tensor_copy(
                out=x_sorted[i][:], in_=words.rearrange("p (g w u) -> p g u w", g=X_PASSES, u=2)
            )

        def transpose_x(i):
            xt = psum.tile([P, X_PASSES, 2, P], F32, tag=SETS[i // 4], name="xt")
            words = x_sb[:, SLOTS[i], :].bitcast(F32)
            half = K_PASS // 2
            for g in range(X_PASSES):
                for u in range(2):
                    if i in x_sorted:
                        nc.tensor.transpose(xt[:, g, u, :], x_sorted[i][:, g, u, :], ident_f32[:])
                    else:
                        nc.tensor.transpose(
                            xt[:, g, u, :], words[:, g * half + u : (g + 1) * half : 2], ident_f32[:]
                        )
            return xt

        def group_x(i, xt, copy):
            grouped = stage.tile([P, D], BF16, align_bytes=64, tag="x_grouped")
            copy(
                out=grouped[:].bitcast(F32).rearrange("p (g r u) -> p g r u", g=X_PASSES, u=2),
                in_=xt[:].rearrange("p g u r -> p g r u"),
            )
            return grouped

        def quantise_x(i, grouped):
            cols = slice(i * X_PASSES * P, (i + 1) * X_PASSES * P)
            nc.vector.quantize_mx(
                out=x_codes[:, cols].bitcast(FP8X4), scales=x_scales[:, cols], in_=grouped[:]
            )

        def x_pass(i, g):
            cols = slice((i * X_PASSES + g) * P, (i * X_PASSES + g + 1) * P)
            return x_codes[:, cols], x_scales[:, cols]

        def sort_proj_codes():
            nc.vector.tensor_copy(
                out=proj_w[:].bitcast(I32),
                in_=proj_raw[:].bitcast(I32).rearrange("p g (m t) -> p g t m", t=PACK),
            )

        def sort_proj_scales():
            by_t = proj_raw_scales[:].rearrange("p (g m t) -> p t g m", g=X_PASSES, t=PACK)
            for t in range(PACK):
                nc.vector.tensor_copy(out=proj_scales[:, :, t, :], in_=by_t[:, t, :, :])

        def project(i, ring=1):
            h_ps = psum.tile([P, PACK, P], F32, tag=SETS[ring], name="h_ps")
            for t in range(PACK):
                for g in range(X_PASSES):
                    codes, scales = x_pass(i, g)
                    nc.tensor.matmul_mx(
                        out=h_ps[:, t, :],
                        lhsT=proj_w[:, g, t, :].bitcast(FP8X4),
                        lhsT_scale=proj_scales[:, g, t, :],
                        rhs=codes.bitcast(FP8X4),
                        rhs_scale=scales,
                        start=(g == 0),
                        stop=(g == X_PASSES - 1),
                    )
            return h_ps

        def round_h(i, h_ps, grouped, copy):
            copy(out=grouped[:, i % 2, :, :], in_=h_ps[:].rearrange("p t r -> p r t"))

        def quantise_h(j, grouped):
            cols = slice(2 * j * P, 2 * (j + 1) * P)
            nc.vector.quantize_mx(
                out=h_codes[:, cols].bitcast(FP8X4),
                scales=h_scales[:, cols],
                in_=grouped[:].rearrange("p a r t -> p (a r t)"),
            )

        def passes_of(kind, i):
            if kind == "head":
                return [
                    x_pass(i, g) + (head_w[:, g, :], head_planes[HEAD_PLANE[g] : P, :]) for g in range(X_PASSES)
                ]
            cols = slice(i * P, (i + 1) * P)
            return [(h_codes[:, cols], h_scales[:, cols], tail_w[:], tail_plane[:])]

        def logits_bank(passes, c, bank_set):
            cols = slice(c * BANK, (c + 1) * BANK)
            bank = psum.tile([P, BANK], F32, tag=bank_set, name="bank")
            for k, (codes, scales, w_words, w_scales) in enumerate(passes):
                nc.tensor.matmul_mx(
                    out=bank[:],
                    lhsT=codes.bitcast(FP8X4),
                    lhsT_scale=scales,
                    rhs=w_words[:, cols].bitcast(FP8X4),
                    rhs_scale=w_scales[:, cols],
                    start=(k == 0),
                    stop=(k == len(passes) - 1),
                )
            return bank

        def exponential(bank, c, minus_max, first_col, bank_sum):
            nc.scalar.activation(
                out=out_sb[:, first_col + c * BANK : first_col + (c + 1) * BANK],
                in_=bank[:],
                func=ACT.Exp,
                bias=minus_max[:],
                accum_out=bank_sum[:, c : c + 1],
            )

        order = [("head", 0)]
        for i in range(TILES - 1):
            order.extend([("head", i + 1), ("tail", i)])
        order.append(("tail", TILES - 1))
        softmaxes = len(order)
        banks = {}
        minus_max = {}
        sums = {}
        inverse = {}

        def first_col(u):
            kind, i = order[u]
            return SLOTS[i] * SPAN + (0 if kind == "head" else VOCAB)

        def cluster_of(u):
            kind, i = order[u]
            col = SLOTS[i] * SPAN + HEAD_TOKENS
            return None if kind == "head" else out_sb[:, col : col + 1]

        def store(u, lo, hi, queue=nc.sync):
            kind, i = order[u]
            at = SLOTS[i] * ROW + (0 if kind == "head" else HEAD_TOKENS)
            first = first_col(u)
            hi = min(hi, HEAD_TOKENS) if kind == "head" else hi
            queue.dma_start(out=probs[:, at + lo : at + hi], in_=out_sb[:, first + lo : first + hi])

        def fill(u, c):
            banks.setdefault(u, []).append(logits_bank(passes_of(*order[u]), c, SETS[u % 2]))

        def scale_rows(u, pieces=1):
            first, cols, cluster = first_col(u), VOCAB // pieces, cluster_of(u)
            for k in range(pieces):
                part = out_sb[:, first + k * cols : first + (k + 1) * cols]
                nc.gpsimd.tensor_scalar(
                    out=part,
                    in0=part,
                    scalar1=inverse[u][:],
                    scalar2=0.0 if cluster is None else cluster,
                    op0=ALU.mult,
                    op1=ALU.add if cluster is None else ALU.mult,
                )
                store(u, k * cols, (k + 1) * cols)

        def scale_piece_on_vector(u, c, cols=BANK):
            first, cluster = first_col(u), cluster_of(u)
            part = out_sb[:, first + c * cols : first + (c + 1) * cols]
            nc.vector.tensor_scalar(
                out=part,
                in0=part,
                scalar1=inverse[u][:],
                scalar2=1.0 if cluster is None else cluster,
                op0=ALU.mult,
                op1=ALU.mult,
            )
            store(u, c * cols, (c + 1) * cols)

        def bank_maximum(u, c):
            if c == 0:
                bank_max[u] = small.tile([P, ROW_BANKS], F32, tag="bank_max", name="bank_max")
            nc.vector.reduce_max(out=bank_max[u][:, c : c + 1], in_=banks[u][c][:], axis=AXIS.X)

        def row_maximum(u):
            minus_max[u] = small.tile([P, 1], F32, tag="minus_max", name="minus_max")
            nc.vector.tensor_reduce(
                out=minus_max[u][:], in_=bank_max[u][:], axis=AXIS.X, op=ALU.max, negate=True
            )

        def row_sum(u):
            totals[u] = small.tile([P, 1], F32, tag="total", name="total")
            nc.vector.reduce_sum(out=totals[u][:], in_=sums[u][:], axis=AXIS.X)

        def invert_sum(u):
            inverse[u] = small.tile([P, 1], F32, tag="inverse", name="inverse")
            nc.vector.reciprocal(out=inverse[u][:], in_=totals[u][:])

        bank_max = {}
        totals = {}
        idle = psum.tile([P, BANK], F32, tag=SETS[1], name="idle")
        for k in range(WARM_UP):
            nc.tensor.matmul(out=idle[:], lhsT=warm[:, 0:P], rhs=warm[:], start=True, stop=True)
        x_grouped = {}
        h_grouped = {}

        def make_h(i, copy):
            if i % 2 == 0:
                h_grouped[i // 2] = stage.tile([P, 2, P, PACK], BF16, align_bytes=64, tag="h_grouped", name="h_grouped")
            round_h(i, project(i), h_grouped[i // 2], copy)

        AHEAD = 3
        sort_proj_codes()
        for i in range(AHEAD):
            sort_words(i)
            if i == 1:
                sort_proj_scales()

        def prepare_x(i):
            x_grouped[i] = group_x(i, transpose_x(i), nc.scalar.copy)
            if i == 1:
                for k in range(2):
                    nc.tensor.matmul(out=idle[:, 0:384], lhsT=warm[:, 0:P], rhs=warm[:, 0:384], start=True, stop=True)
            if i >= 1:
                quantise_x(i - 1, x_grouped[i - 1])
            if i + AHEAD < TILES:
                sort_words(i + AHEAD)

        for i in range(4):
            prepare_x(i)
        make_h(0, nc.scalar.copy)
        make_h(1, nc.scalar.copy)
        for i in range(4, TILES):
            prepare_x(i)
            if i == 4:
                quantise_h(0, h_grouped[0])
        quantise_x(TILES - 1, x_grouped[TILES - 1])
        make_h(2, nc.scalar.copy)
        make_h(3, nc.scalar.copy)
        make_h(4, nc.scalar.copy)
        quantise_h(1, h_grouped[1])
        make_h(5, nc.scalar.copy)
        for c in range(ROW_BANKS):
            fill(0, c)
            bank_maximum(0, c)
        row_maximum(0)
        quantise_h(2, h_grouped[2])
        for c in range(ROW_BANKS):
            fill(1, c)
        bank_maximum(1, 0)
        last_h = []
        for u in range(softmaxes):
            sums[u] = small.tile([P, ROW_BANKS], F32, tag="sums", name="sums")
            for c in range(ROW_BANKS):
                exponential(banks[u][c], c, minus_max[u], first_col(u), sums[u])
                if u == 0 and c < 2:
                    last_h.append(project(6 + c, 0))
                elif u + 2 < softmaxes:
                    fill(u + 2, c - 2 if u == 0 else c)
            if u == 0:
                h_grouped[3] = stage.tile([P, 2, P, PACK], BF16, align_bytes=64, tag="h_grouped", name="h_grouped")
                for c in range(2):
                    round_h(6 + c, last_h[c], h_grouped[3], nc.scalar.copy)
                    fill(2, 2 + c)
            if u + 1 < softmaxes:
                bank_maximum(u + 1, 1)
            if u >= 1:
                row_sum(u - 1)
            if u + 1 < softmaxes:
                bank_maximum(u + 1, 2)
            if u == 1:
                quantise_h(3, h_grouped[3])
            if u >= 1:
                invert_sum(u - 1)
            if u + 1 < softmaxes:
                bank_maximum(u + 1, 3)
            if u == 0:
                row_maximum(u + 1)
            if u + 2 < softmaxes:
                bank_maximum(u + 2, 0)
            if 1 <= u < softmaxes - 1:
                row_maximum(u + 1)
            if 1 <= u < softmaxes - (3 - 1):
                scale_rows(u - 1, 2 if u - 1 >= 11 else 1)
            elif u >= 1:
                scale_piece_on_vector(u - 1, 0, VOCAB)

        nc.gpsimd.tensor_copy(out=others[:], in_=out_sb[:, VOCAB - 1 : TILES * SPAN : SPAN])
        nc.sync.dma_start(out=other_cluster, in_=others[:])
        u = softmaxes - 1
        row_sum(u)
        invert_sum(u)
        factor = small.tile([P, 1], F32)
        nc.scalar.activation(out=factor[:], in_=inverse[u][:], func=ACT.Copy, scale=cluster_of(u))
        scale_piece_on_vector(u, 0, 2 * BANK)
        scale_piece_on_vector(u, 2)
        lo = first_col(u) + 3 * BANK
        nc.scalar.activation(out=out_sb[:, lo : lo + BANK], in_=out_sb[:, lo : lo + BANK], func=ACT.Copy, scale=factor[:])
        store(u, 3 * BANK, VOCAB, nc.scalar)
